import numpy as np
import ml_dtypes


def mxq(x, axis, fmt="e4m3"):
    dtype, down = {"e4m3": (ml_dtypes.float8_e4m3fn, 7), "e5m2": (ml_dtypes.float8_e5m2, 14)}[fmt]
    v = np.moveaxis(np.asarray(x, np.float32).astype(ml_dtypes.bfloat16).astype(np.float64), axis, -1)
    blocks = v.reshape(v.shape[:-1] + (-1, 32))
    amax = np.abs(blocks).max(-1, keepdims=True)
    byte = np.maximum(np.where(amax > 0, np.frexp(amax)[1] - 1 + 127, 0) - down, 1)
    scale = np.exp2(byte - 127.0)
    codes = (blocks / scale).astype(np.float32).astype(dtype).astype(np.float64)
    return np.moveaxis((codes * scale).reshape(v.shape), -1, axis)


WIDE = False


def mx_kscale(k):
    if not WIDE:
        return np.ones(k)
    levels = np.array([18, -18])
    if k % 512:
        return np.exp2(np.random.permutation(np.resize(levels, k // 32))).repeat(32)
    a = np.empty((k // 512, 16))
    for p in range(k // 512):
        a[p, :8] = np.random.permutation(np.resize(levels, 8))
        for g in range(8):
            far = levels[np.abs(levels - a[p, g]) >= 10]
            a[p, g + 8] = far[np.random.randint(len(far))]
    return np.exp2(a.ravel()).repeat(32)


BF16 = ml_dtypes.bfloat16


def bf(x):
    return np.asarray(x, np.float32).astype(BF16)


def f64(x):
    return np.asarray(x).astype(np.float64)


B, E, C, K, H = 8, 512, 512, 2, 512
EPS = 1e-5
SA = np.sqrt(6.0 / (E + E))


def adjacency(adj, adj_bias):
    return np.maximum(f64(adj) + f64(adj_bias), 0.0)


def setup_inputs():
    s = mx_kscale(C)
    u = mx_kscale(H)
    v = mx_kscale(E)
    m = np.min(v) / v
    r = np.ones((K * C, H))
    r[1::K] = 1.0 / (s[:, None] * u)
    x0 = bf(np.random.standard_normal((B, E, C)) + np.random.standard_normal((B, 1, C)))
    adj0 = f64(bf(np.random.standard_normal((E, E)) * SA))
    adj_bias = bf(SA * (-1.0 + 0.1 * np.random.standard_normal(1)))
    adj0 = np.where(adj0 + f64(adj_bias) == 0.0, 0.0, adj0)
    cw0 = bf(np.random.standard_normal((K * C, H)) * np.sqrt(6.0 / (K * C + H)))
    brelu_bias = bf(np.random.standard_normal((1, 1, H)) * 0.2)
    g = bf(np.random.standard_normal((B, E, H)) * np.exp2(np.random.randint(-6, 1, (B, E, 1))) * m[:, None] * u)
    w = adjacency(adj0, adj_bias)
    d = 1.0 / np.sqrt(w.sum(axis=1) + EPS)
    lap = np.eye(E) - d[:, None] * w * d[None, :]
    cf = f64(cw0)
    z = f64(brelu_bias) + cf[0::K].sum(axis=0) + (lap @ f64(x0)) @ cf[1::K]
    return {"x": bf(f64(x0) * s),
            "adj": bf(adj0 / m[:, None]),
            "adj_bias": adj_bias,
            "cheb_w": bf(cf * r),
            "brelu_bias": brelu_bias,
            "z": np.asarray(z, np.float32),
            "d": np.asarray(d, np.float32),
            "grad_out": g}


def reference(x, adj, adj_bias, cheb_w, brelu_bias, z, d, grad_out):
    w = adjacency(adj, adj_bias)
    df = f64(d)
    dz2 = f64(grad_out) * (f64(z) > 0.0)
    dt1 = mxq(dz2, 2, "e5m2") @ mxq(f64(cheb_w)[1::K], 1, "e4m3").T
    dz1 = -df[:, None] * dt1
    dx = dt1 + df[:, None] * (mxq(w, 0, "e4m3").T @ mxq(dz1, 1, "e5m2"))
    gt = dz1.transpose(1, 0, 2).reshape(E, B * C)
    xt = f64(x).transpose(1, 0, 2).reshape(E, B * C)
    p = mxq(gt, 1, "e5m2") @ mxq(xt, 1, "e4m3").T
    pw = p * w
    rs = (pw * df[None, :]).sum(axis=1)
    cs = pw.sum(axis=0)
    dw = p * df[None, :] - (0.5 * df ** 2 * rs + 0.5 * df ** 3 * cs)[:, None]
    dadj = dw * (f64(adj) + f64(adj_bias) > 0.0)
    return dx, dadj

@@ -1,0 +1,515 @@
+from contextlib import ExitStack
+
+import concourse.mybir as mybir
+from concourse.masks import make_identity
+
+B, N = 8, 512
+P = 128
+T = 4
+HALVES = 2
+HALF = N * T // HALVES
+
+FLOPS = 3 * 2 * B * N * N * N
+BYTES = B * N * N * (2 + 2 + 4 + 4) + N * N * (2 + 2 + 4) + N * 4 + 2
+
+F32 = mybir.dt.float32
+BF16 = mybir.dt.bfloat16
+U32 = mybir.dt.uint32
+U8 = mybir.dt.uint8
+E4M3 = mybir.dt.float8_e4m3fn_x4
+E5M2 = mybir.dt.float8_e5m2_x4
+ALU = mybir.AluOpType
+ACT = mybir.ActivationFunctionType
+
+P_IN_LOOP = 2
+SCALE_ENGINE = "vvvv"
+VECTOR_SHARE = (64, 0, 0, 0, 0, 0, 64, 0)
+
+
+def tile_brainfunctionalconnectivityfeatureextrac_pa_v_kernel(
+    tc, x, adj, adj_bias, cheb_w, brelu_bias, z, d, grad_out, out_0, out_1
+):
+    nc = tc.nc
+    with ExitStack() as ctx:
+        keep = ctx.enter_context(tc.tile_pool(name="keep", bufs=1))
+        load = ctx.enter_context(tc.tile_pool(name="load", bufs=3))
+        work = ctx.enter_context(tc.tile_pool(name="work", bufs=2))
+        psum = ctx.enter_context(tc.psum_pool(name="psum", bufs=1))
+        ctx.enter_context(tc.manual_schedule())
+
+        def bank(name, shape):
+            return psum.tile(shape, F32, name=name, tag="scalar_side", bufs=6 - P_IN_LOOP)
+
+        def held_bank(name, shape):
+            return psum.tile(shape, F32, name=name, tag="p_held", bufs=P_IN_LOOP)
+
+        def mx_pair(pool, name, tag, bufs):
+            codes = pool.tile([P, N], U32, name=name + "_codes", tag=tag + "_codes", bufs=bufs, align_bytes=64)
+            scales = pool.tile([P, N], U8, name=name + "_scales", tag=tag + "_scales", bufs=bufs, align_bytes=64)
+            return codes, scales
+
+        def quantize(pair, fmt, grouped):
+            nc.vector.quantize_mx(out=pair[0][:].bitcast(fmt), scales=pair[1][:], in_=grouped[:])
+
+        def mx_pass(acc, lhs, lhs_fmt, tile_index, rhs, rhs_fmt, start, stop):
+            cols = slice(tile_index * P, (tile_index + 1) * P)
+            nc.tensor.matmul_mx(
+                out=acc,
+                lhsT=lhs[0][:, cols].bitcast(lhs_fmt),
+                lhsT_scale=lhs[1][:, cols],
+                rhs=rhs[0][:].bitcast(rhs_fmt),
+                rhs_scale=rhs[1][:],
+                start=start,
+                stop=stop,
+            )
+
+        def grouped_tile(tag):
+            return work.tile([P, N * T], BF16, name=tag, tag=tag, bufs=2, align_bytes=64)
+
+        ident = keep.tile([P, P], F32, name="ident")
+        make_identity(nc, ident[:])
+        ones = keep.tile([P, 2], F32, name="ones")
+        nc.gpsimd.memset(ones[:], 1.0)
+
+        g_half, z_half, x_rows = {}, {}, {}
+        sorted_half, g_grouped, g_mx = {}, {}, {}
+        dt1, dz1, z_banks = {}, {}, {}
+        zt_grouped, xt_grouped, zt_mx, xt_mx = {}, {}, {}, {}
+        a_grouped, a_mx, u_banks, p_banks = {}, {}, {}, {}
+
+        def load_gz(b):
+            for h in range(HALVES):
+                cols = slice(h * HALF, (h + 1) * HALF)
+                g_half[b, h] = load.tile([P, HALF], BF16, name="g_half", tag="g_half", bufs=6)
+                nc.sync.dma_start(out=g_half[b, h][:], in_=grad_out[b].rearrange("(p t) h -> p (t h)", t=T)[:, cols])
+                z_half[b, h] = load.tile([P, HALF], F32, name="z_half", tag="z_half", bufs=6)
+                nc.sync.dma_start(out=z_half[b, h][:], in_=z[b].rearrange("(p t) h -> p (t h)", t=T)[:, cols])
+
+        def load_x(b):
+            x_rows[b] = load.tile([P, N * T], BF16, name="x_rows", tag="x_rows", bufs=3)
+            nc.sync.dma_start(out=x_rows[b][:], in_=x[b].rearrange("(p t) c -> p (t c)", t=T))
+
+        def by_run(ap):
+            return ap.rearrange("p (a u r) -> p u a r", u=2, r=16)
+
+        def sorted_view(ap):
+            return ap.rearrange("p (u a r) -> p u a r", u=2, r=16)
+
+        def new_sorted_half(key):
+            sorted_half[key] = work.tile([P, HALF], BF16, name="sorted_half", tag="sorted_half", bufs=4)
+            return sorted_half[key]
+
+        def mask_grad(b, h):
+            dst = new_sorted_half((b, h))
+            for u in range(2):
+                nc.vector.scalar_tensor_tensor(
+                    out=sorted_view(dst[:])[:, u],
+                    in0=by_run(z_half[b, h][:])[:, u],
+                    scalar=0.0,
+                    in1=by_run(g_half[b, h][:])[:, u],
+                    op0=ALU.is_gt,
+                    op1=ALU.mult,
+                )
+
+        def transpose_sorted(key):
+            words = sorted_half[key][:].bitcast(F32)
+            acc = bank("sorted_t", [P, 4, P])
+            for t in range(2):
+                for u in range(2):
+                    first = (2 * u + t) * P
+                    nc.tensor.transpose(acc[:, 2 * t + u, :], words[:, first : first + P], ident[:])
+            return acc
+
+        def copy_tiles_apart(grouped, h, acc):
+            words = grouped[:].bitcast(F32)[:, h * N : (h + 1) * N]
+            nc.scalar.copy(
+                out=words.rearrange("q (t p u) -> q t p u", t=2, u=2),
+                in_=acc[:].rearrange("q (t u) p -> q t p u", u=2),
+            )
+
+        def transpose_rows(rows, h):
+            words = rows[:].bitcast(F32)
+            acc = bank("rows_t", [P, 4, P])
+            for t in range(2):
+                for u in range(2):
+                    first = (2 * h + t) * 2 * P
+                    nc.tensor.transpose(acc[:, 2 * t + u, :], words[:, first + u : first + 2 * P : 2], ident[:])
+            return acc
+
+        def copy_rows_in_order(grouped, h, acc):
+            words = grouped[:].bitcast(F32).rearrange("q (p h s) -> q h p s", h=2, s=4)
+            nc.scalar.copy(out=words[:, h], in_=acc[:].rearrange("q s p -> q p s"))
+
+        def grad_to_features(b, h):
+            acc = transpose_sorted((b, h))
+            if h == 0:
+                g_grouped[b] = grouped_tile("g_grouped")
+            copy_tiles_apart(g_grouped[b], h, acc)
+
+        def quantize_grad(b):
+            g_mx[b] = mx_pair(work, "g", "g", 2)
+            quantize(g_mx[b], E5M2, g_grouped[b])
+
+        def tile_cols(t):
+            return slice(t * N, (t + 1) * N)
+
+        def first_product(b, t):
+            if t == 0:
+                dt1[b] = work.tile([P, T * N], F32, name="rows_f32", tag="rows_f32", bufs=4)
+                dz1[b] = work.tile([P, T * N], BF16, name="dz1", tag="dz1", bufs=3)
+            acc = bank("dt1_acc", [P, N])
+            mx_pass(acc[:], g_mx[b], E5M2, t, w1_mx, E4M3, True, True)
+            nc.scalar.copy(out=dt1[b][:, tile_cols(t)], in_=acc[:])
+            dst = dz1[b][:, tile_cols(t)].rearrange("p (u w e) -> p u w e", u=2, e=2)
+            if scale_engine(b, t) == "s":
+                nc.scalar.activation(
+                    out=dst,
+                    in_=acc[:].rearrange("p (w u e) -> p u w e", u=2, e=2),
+                    func=ACT.Copy,
+                    scale=neg_d[:, t : t + 1],
+                )
+            if scale_engine(b, t) == "g":
+                nc.gpsimd.tensor_scalar(
+                    out=dst,
+                    in0=dt1[b][:, tile_cols(t)].rearrange("p (w u e) -> p u w e", u=2, e=2),
+                    scalar1=neg_d[:, t : t + 1],
+                    scalar2=0.0,
+                    op0=ALU.mult,
+                    op1=ALU.add,
+                )
+
+        def scale_engine(b, t):
+            return SCALE_ENGINE[t]
+
+        def scale_rows(b, h):
+            for t in (2 * h, 2 * h + 1):
+                if scale_engine(b, t) == "v":
+                    nc.vector.tensor_scalar(
+                        out=dz1[b][:, tile_cols(t)].rearrange("p (u w e) -> p u w e", u=2, e=2),
+                        in0=dt1[b][:, tile_cols(t)].rearrange("p (w u e) -> p u w e", u=2, e=2),
+                        scalar1=neg_d[:, t : t + 1],
+                        scalar2=None,
+                        op0=ALU.mult,
+                    )
+
+        def transpose_dz1(b, h):
+            words = dz1[b][:].bitcast(F32)
+            z_banks[b, h] = bank("dz1_t", [P, 4, P])
+            for s in range(4):
+                first = (4 * h + s) * P
+                nc.tensor.transpose(z_banks[b, h][:, s, :], words[:, first : first + P], ident[:])
+
+        def copy_dz1_t(b, h):
+            if h == 0:
+                zt_grouped[b] = grouped_tile("zt_grouped")
+            copy_rows_in_order(zt_grouped[b], h, z_banks[b, h])
+
+        def quantize_dz1_t(b):
+            zt_mx[b] = mx_pair(keep, "zt", "zt", B)
+            quantize(zt_mx[b], E5M2, zt_grouped[b])
+
+        def x_to_channels(b, h):
+            acc = transpose_rows(x_rows[b], h)
+            if h == 0:
+                xt_grouped[b] = grouped_tile("xt_grouped")
+            copy_rows_in_order(xt_grouped[b], h, acc)
+
+        def quantize_x_t(b):
+            xt_mx[b] = mx_pair(keep, "xt", "xt", B)
+            quantize(xt_mx[b], E4M3, xt_grouped[b])
+
+        def interleave_views(b, first, last):
+            src = dz1[b][:].rearrange("p (t u w e) -> p u w t e", t=T, u=2, e=2)[:, :, first:last]
+            dst = a_grouped[b][:].rearrange("p (w u e t) -> p u w t e", t=T, u=2, e=2)[:, :, first:last]
+            return dst, src
+
+        def interleave_on_scalar(b, h):
+            if h == 0:
+                a_grouped[b] = grouped_tile("a_grouped")
+            middle = (VECTOR_SHARE[b] + P) // 2
+            dst, src = interleave_views(b, VECTOR_SHARE[b], middle) if h == 0 else interleave_views(b, middle, P)
+            nc.scalar.copy(out=dst, in_=src)
+
+        def interleave_on_vector(b):
+            if VECTOR_SHARE[b] > 0:
+                dst, src = interleave_views(b, 0, VECTOR_SHARE[b])
+                nc.vector.tensor_copy(out=dst, in_=src)
+
+        def quantize_dz1(b):
+            a_mx[b] = mx_pair(work, "a", "a", 2)
+            quantize(a_mx[b], E5M2, a_grouped[b])
+
+        def mix_nodes(b, t):
+            u_banks[b, t] = psum.tile([P, N], F32, name="u_acc", tag="vector_side", bufs=2)
+            mx_pass(u_banks[b, t][:], w_mx, E4M3, t, a_mx[b], E5M2, True, True)
+
+        def finish_dx(b, t):
+            nc.vector.scalar_tensor_tensor(
+                out=dt1[b][:, tile_cols(t)],
+                in0=u_banks[b, t][:],
+                scalar=d_by4[:, t : t + 1],
+                in1=dt1[b][:, tile_cols(t)],
+                op0=ALU.mult,
+                op1=ALU.add,
+            )
+            if t % 2 == 1:
+                cols = slice((t - 1) * N, (t + 1) * N)
+                nc.sync.dma_start(out=out_0[b].rearrange("(p t) c -> p (t c)", t=T)[:, cols], in_=dt1[b][:, cols])
+
+        def p_pass(r, b):
+            if b == 0:
+                if r < P_IN_LOOP:
+                    p_banks[r] = held_bank("p_held", [P, N])
+                else:
+                    p_banks[r] = bank("p_acc", [P, N])
+            mx_pass(p_banks[r][:], xt_mx[b], E4M3, r, zt_mx[b], E5M2, b == 0, b == B - 1)
+
+        w1_rows = keep.tile([P, T, N], BF16, name="w1_rows")
+        nc.sync.dma_start(out=w1_rows[:], in_=cheb_w.rearrange("(r p k) h -> k p r h", k=2, p=P)[1])
+        load_gz(0)
+        d_by4 = keep.tile([P, T], F32, name="d_by4")
+        nc.sync.dma_start(out=d_by4[:], in_=d.rearrange("(p t) -> p t", t=T))
+        bias = keep.tile([P, 1], BF16, name="bias")
+        with nc.allow_non_contiguous_dma(reason="one number for every partition"):
+            nc.sync.dma_start(out=bias[:], in_=adj_bias.partition_broadcast(P))
+        adj_by4 = keep.tile([P, T * N], BF16, name="adj_by4")
+        nc.sync.dma_start(out=adj_by4[:], in_=adj.rearrange("(p t) j -> p (t j)", t=T))
+        load_gz(1)
+        load_x(0)
+        load_x(1)
+        adj_rows = keep.tile([P, T, N], BF16, name="adj_rows")
+        nc.sync.dma_start(out=adj_rows[:], in_=adj.rearrange("(r p) j -> p r j", p=P))
+        load_gz(2)
+
+        w1_flat = w1_rows[:].rearrange("p r h -> p (r h)")
+        w1_grouped = grouped_tile("a_grouped")
+        for h in range(HALVES):
+            dst = new_sorted_half(("w1", h))
+            nc.vector.tensor_copy(out=sorted_view(dst[:]), in_=by_run(w1_flat[:, h * HALF : (h + 1) * HALF]))
+        for h in range(HALVES):
+            copy_tiles_apart(w1_grouped, h, transpose_sorted(("w1", h)))
+        mask_grad(0, 0)
+        mask_grad(0, 1)
+        w1_mx = mx_pair(keep, "w1", "w1", 1)
+        quantize(w1_mx, E4M3, w1_grouped)
+        neg_d = keep.tile([P, T], F32, name="neg_d")
+        nc.vector.tensor_scalar(out=neg_d[:], in0=d_by4[:], scalar1=-1.0, scalar2=None, op0=ALU.mult)
+        grad_to_features(0, 0)
+        grad_to_features(0, 1)
+
+        w_mx = mx_pair(keep, "w", "w", 1)
+        w_t = keep.tile([P, T, N], F32, name="w_t")
+        mask = keep.tile([P, T, N], BF16, name="mask")
+        d_rows = keep.tile([P, T], F32, name="d_rows")
+        factor = keep.tile([P, T], F32, name="factor")
+        ident_bf = keep.tile([P, P], BF16, name="ident_bf")
+        make_identity(nc, ident_bf[:])
+
+        def transpose_w(s):
+            acc = psum.tile([P, T, P], BF16, name="adj_t", tag="scalar_side", bufs=6 - P_IN_LOOP)
+            for r in range(T):
+                nc.tensor.transpose(acc[:, r, :], adj_rows[:, r, s * P : (s + 1) * P], ident_bf[:])
+            nc.scalar.activation(
+                out=w_t[:, s, :], in_=acc[:].rearrange("p r m -> p (r m)"), func=ACT.Relu, bias=bias[:]
+            )
+
+        last = B - 1
+        g_mx[0] = mx_pair(work, "g", "g", 2)
+        for h in range(HALVES):
+            cols = slice(h * N // 2, (h + 1) * N // 2)
+            nc.vector.quantize_mx(
+                out=g_mx[0][0][:, cols].bitcast(E5M2),
+                scales=g_mx[0][1][:, cols],
+                in_=g_grouped[0][:, h * HALF : (h + 1) * HALF],
+            )
+        for k in range(last):
+            if k + 2 < B:
+                load_x(k + 2)
+            if k + 3 < B:
+                load_gz(k + 3)
+            if k == 2:
+                with nc.allow_non_contiguous_dma(reason="one factor for each row"):
+                    nc.sync.dma_start(out=d_rows[:], in_=d.rearrange("(r p) -> p r", p=P))
+            if k >= 1:
+                copy_dz1_t(k - 1, 0)
+                copy_dz1_t(k - 1, 1)
+            first_product(k, 0)
+            first_product(k, 1)
+            mask_grad(k + 1, 0)
+            grad_to_features(k + 1, 0)
+            if k >= 1:
+                quantize_x_t(k)
+                quantize_dz1_t(k - 1)
+            first_product(k, 2)
+            first_product(k, 3)
+            if k >= 2:
+                finish_dx(k - 2, 0)
+                mix_nodes(k - 2, 2)
+            scale_rows(k, 0)
+            if k >= 2:
+                finish_dx(k - 2, 1)
+                mix_nodes(k - 2, 3)
+            if k == 0:
+                w_grouped = grouped_tile("a_grouped")
+                nc.vector.tensor_scalar(
+                    out=w_grouped[:].rearrange("p (s m t) -> p s m t", s=T, t=T),
+                    in0=adj_by4[:].rearrange("p (t m s) -> p s m t", s=T, t=T),
+                    scalar1=bias[:],
+                    scalar2=0.0,
+                    op0=ALU.add,
+                    op1=ALU.max,
+                )
+                x_to_channels(0, 0)
+                x_to_channels(0, 1)
+            else:
+                interleave_on_scalar(k - 1, 0)
+                interleave_on_scalar(k - 1, 1)
+            mask_grad(k + 1, 1)
+            scale_rows(k, 1)
+            if k >= 1:
+                interleave_on_vector(k - 1)
+            grad_to_features(k + 1, 1)
+            x_to_channels(k + 1, 0)
+            if k >= 1:
+                p_pass(0, k - 1)
+                p_pass(1, k - 1)
+            x_to_channels(k + 1, 1)
+            transpose_dz1(k, 0)
+            transpose_dz1(k, 1)
+            if k >= 2:
+                finish_dx(k - 2, 2)
+                finish_dx(k - 2, 3)
+            if k == 1:
+                nc.vector.tensor_scalar(
+                    out=mask[:], in0=adj_rows[:], scalar1=bias[:], scalar2=0.0, op0=ALU.add, op1=ALU.is_gt
+                )
+            if k == 3:
+                nc.vector.scalar_tensor_tensor(
+                    out=factor[:], in0=d_rows[:], scalar=-0.5, in1=d_rows[:], op0=ALU.mult, op1=ALU.mult
+                )
+            if k >= 1:
+                quantize_dz1(k - 1)
+                mix_nodes(k - 1, 0)
+                mix_nodes(k - 1, 1)
+            else:
+                quantize(w_mx, E4M3, w_grouped)
+                quantize_x_t(0)
+            quantize_grad(k + 1)
+
+        col_sums = keep.tile([P, T], F32, name="col_sums")
+        row_sums = keep.tile([P, T], F32, name="row_sums")
+        both_sums = keep.tile([P, T], F32, name="both_sums")
+        shift = keep.tile([P, T], F32, name="shift")
+        p_d = keep.tile([P, T, N], F32, name="p_d")
+        p_wd = keep.tile([P, T, N], F32, name="p_wd")
+        pd_banks = {}
+
+        def scale_p(s):
+            nc.scalar.activation(out=p_d[:, s, :], in_=p_banks[s][:], func=ACT.Copy, scale=d_rows[:, s : s + 1])
+
+        def weigh_p(s):
+            nc.vector.scalar_tensor_tensor(
+                out=p_wd[:, s, :],
+                in0=p_banks[s][:],
+                scalar=d_rows[:, s : s + 1],
+                in1=w_t[:, s, :],
+                op0=ALU.mult,
+                op1=ALU.mult,
+                accum_out=col_sums[:, s : s + 1],
+            )
+
+        def sum_rows(s):
+            for r in range(T):
+                nc.tensor.matmul(
+                    out=row_parts[:, r, s, :], lhsT=p_wd[:, s, r * P : (r + 1) * P], rhs=ones[:], start=True, stop=True
+                )
+
+        def transpose_back(r):
+            pd_banks[r] = held_bank("pd_held", [P, T, P]) if r < P_IN_LOOP else bank("pd_acc", [P, T, P])
+            for s in range(T):
+                nc.tensor.transpose(pd_banks[r][:, s, :], p_d[:, s, r * P : (r + 1) * P], ident[:])
+
+        copy_dz1_t(last - 1, 0)
+        copy_dz1_t(last - 1, 1)
+        first_product(last, 0)
+        first_product(last, 1)
+        finish_dx(last - 2, 0)
+        quantize_x_t(last)
+        finish_dx(last - 2, 1)
+        quantize_dz1_t(last - 1)
+        first_product(last, 2)
+        first_product(last, 3)
+        mix_nodes(last - 2, 2)
+        mix_nodes(last - 2, 3)
+        transpose_w(0)
+        transpose_w(1)
+        scale_rows(last, 0)
+        transpose_dz1(last, 0)
+        p_pass(0, last - 1)
+        p_pass(1, last - 1)
+        finish_dx(last - 2, 2)
+        scale_rows(last, 1)
+        transpose_dz1(last, 1)
+        finish_dx(last - 2, 3)
+        copy_dz1_t(last, 0)
+        copy_dz1_t(last, 1)
+        interleave_on_scalar(last - 1, 0)
+        interleave_on_scalar(last - 1, 1)
+        interleave_on_vector(last - 1)
+        for b in range(last):
+            p_pass(2, b)
+        transpose_w(2)
+        transpose_w(3)
+        quantize_dz1_t(last)
+        p_pass(0, last)
+        p_pass(1, last)
+        p_pass(2, last)
+        quantize_dz1(last - 1)
+        mix_nodes(last - 1, 0)
+        mix_nodes(last - 1, 1)
+        for b in range(B):
+            p_pass(3, b)
+        interleave_on_scalar(last, 0)
+        interleave_on_scalar(last, 1)
+        weigh_p(0)
+        weigh_p(1)
+        row_parts = bank("row_parts", [P, T, T, 2])
+        finish_dx(last - 1, 0)
+        mix_nodes(last - 1, 2)
+        finish_dx(last - 1, 1)
+        mix_nodes(last - 1, 3)
+        sum_rows(0)
+        sum_rows(1)
+        weigh_p(2)
+        sum_rows(2)
+        weigh_p(3)
+        sum_rows(3)
+        for s in range(T):
+            scale_p(s)
+        interleave_on_vector(last)
+        finish_dx(last - 1, 2)
+        finish_dx(last - 1, 3)
+        quantize_dz1(last)
+        mix_nodes(last, 0)
+        mix_nodes(last, 1)
+        nc.vector.tensor_reduce(out=row_sums[:], in_=row_parts[:, :, :, 0], axis=mybir.AxisListType.X, op=ALU.add)
+        finish_dx(last, 0)
+        mix_nodes(last, 2)
+        nc.vector.tensor_tensor(out=both_sums[:], in0=col_sums[:], in1=row_sums[:], op=ALU.add)
+        finish_dx(last, 1)
+        mix_nodes(last, 3)
+        for r in range(T):
+            transpose_back(r)
+        nc.vector.tensor_tensor(out=shift[:], in0=both_sums[:], in1=factor[:], op=ALU.mult)
+        finish_dx(last, 2)
+        finish_dx(last, 3)
+        for r in range(T):
+            nc.vector.scalar_tensor_tensor(
+                out=p_wd[:, r, :],
+                in0=pd_banks[r][:].rearrange("p s m -> p (s m)"),
+                scalar=shift[:, r : r + 1],
+                in1=mask[:, r, :],
+                op0=ALU.add,
+                op1=ALU.mult,
+            )
+            nc.sync.dma_start(out=out_1[r * P : (r + 1) * P, :], in_=p_wd[:, r, :])

@@ -22,6 +22,9 @@ ALU = mybir.AluOpType
 ACT = mybir.ActivationFunctionType
 
 P_IN_LOOP = 2
+EARLY_PASSES = 5
+WARM = (0, 0)
+HEAD_WARM = (0, 0, 0, 0)
 SCALE_ENGINE = "vvvv"
 VECTOR_SHARE = (64, 0, 0, 0, 0, 0, 64, 0)
 
@@ -99,9 +102,9 @@ def tile_brainfunctionalconnectivityfeatureextrac_pa_v_kernel(
             sorted_half[key] = work.tile([P, HALF], BF16, name="sorted_half", tag="sorted_half", bufs=4)
             return sorted_half[key]
 
-        def mask_grad(b, h):
-            dst = new_sorted_half((b, h))
-            for u in range(2):
+        def mask_grad(b, h, parts=(0, 1)):
+            dst = new_sorted_half((b, h)) if 0 in parts else sorted_half[b, h]
+            for u in parts:
                 nc.vector.scalar_tensor_tensor(
                     out=sorted_view(dst[:])[:, u],
                     in0=by_run(z_half[b, h][:])[:, u],
@@ -111,9 +114,14 @@ def tile_brainfunctionalconnectivityfeatureextrac_pa_v_kernel(
                     op1=ALU.mult,
                 )
 
-        def transpose_sorted(key):
+        def keep_warm(acc, count):
+            for n in range(count):
+                nc.tensor.matmul(out=acc[:, 0, :], lhsT=ident[:], rhs=ident[:], start=True, stop=True)
+
+        def transpose_sorted(key, warm=0):
             words = sorted_half[key][:].bitcast(F32)
             acc = bank("sorted_t", [P, 4, P])
+            keep_warm(acc, warm)
             for t in range(2):
                 for u in range(2):
                     first = (2 * u + t) * P
@@ -127,9 +135,10 @@ def tile_brainfunctionalconnectivityfeatureextrac_pa_v_kernel(
                 in_=acc[:].rearrange("q (t u) p -> q t p u", u=2),
             )
 
-        def transpose_rows(rows, h):
+        def transpose_rows(rows, h, warm=0):
             words = rows[:].bitcast(F32)
             acc = bank("rows_t", [P, 4, P])
+            keep_warm(acc, warm)
             for t in range(2):
                 for u in range(2):
                     first = (2 * h + t) * 2 * P
@@ -140,8 +149,8 @@ def tile_brainfunctionalconnectivityfeatureextrac_pa_v_kernel(
             words = grouped[:].bitcast(F32).rearrange("q (p h s) -> q h p s", h=2, s=4)
             nc.scalar.copy(out=words[:, h], in_=acc[:].rearrange("q s p -> q p s"))
 
-        def grad_to_features(b, h):
-            acc = transpose_sorted((b, h))
+        def grad_to_features(b, h, warm=0):
+            acc = transpose_sorted((b, h), warm)
             if h == 0:
                 g_grouped[b] = grouped_tile("g_grouped")
             copy_tiles_apart(g_grouped[b], h, acc)
@@ -155,7 +164,7 @@ def tile_brainfunctionalconnectivityfeatureextrac_pa_v_kernel(
 
         def first_product(b, t):
             if t == 0:
-                dt1[b] = work.tile([P, T * N], F32, name="rows_f32", tag="rows_f32", bufs=4)
+                dt1[b] = work.tile([P, T * N], F32, name="rows_f32", tag="rows_f32", bufs=5)
                 dz1[b] = work.tile([P, T * N], BF16, name="dz1", tag="dz1", bufs=3)
             acc = bank("dt1_acc", [P, N])
             mx_pass(acc[:], g_mx[b], E5M2, t, w1_mx, E4M3, True, True)
@@ -192,9 +201,10 @@ def tile_brainfunctionalconnectivityfeatureextrac_pa_v_kernel(
                         op0=ALU.mult,
                     )
 
-        def transpose_dz1(b, h):
+        def transpose_dz1(b, h, warm=0):
             words = dz1[b][:].bitcast(F32)
             z_banks[b, h] = bank("dz1_t", [P, 4, P])
+            keep_warm(z_banks[b, h], warm)
             for s in range(4):
                 first = (4 * h + s) * P
                 nc.tensor.transpose(z_banks[b, h][:, s, :], words[:, first : first + P], ident[:])
@@ -208,8 +218,8 @@ def tile_brainfunctionalconnectivityfeatureextrac_pa_v_kernel(
             zt_mx[b] = mx_pair(keep, "zt", "zt", B)
             quantize(zt_mx[b], E5M2, zt_grouped[b])
 
-        def x_to_channels(b, h):
-            acc = transpose_rows(x_rows[b], h)
+        def x_to_channels(b, h, warm=0):
+            acc = transpose_rows(x_rows[b], h, warm)
             if h == 0:
                 xt_grouped[b] = grouped_tile("xt_grouped")
             copy_rows_in_order(xt_grouped[b], h, acc)
@@ -269,18 +279,18 @@ def tile_brainfunctionalconnectivityfeatureextrac_pa_v_kernel(
         load_gz(0)
         d_by4 = keep.tile([P, T], F32, name="d_by4")
         nc.sync.dma_start(out=d_by4[:], in_=d.rearrange("(p t) -> p t", t=T))
+        load_gz(1)
         bias = keep.tile([P, 1], BF16, name="bias")
         with nc.allow_non_contiguous_dma(reason="one number for every partition"):
             nc.sync.dma_start(out=bias[:], in_=adj_bias.partition_broadcast(P))
         adj_by4 = keep.tile([P, T * N], BF16, name="adj_by4")
         nc.sync.dma_start(out=adj_by4[:], in_=adj.rearrange("(p t) j -> p (t j)", t=T))
-        load_gz(1)
         load_x(0)
-        load_x(1)
-        adj_rows = keep.tile([P, T, N], BF16, name="adj_rows")
-        nc.sync.dma_start(out=adj_rows[:], in_=adj.rearrange("(r p) j -> p r j", p=P))
         load_gz(2)
+        load_x(1)
 
+        warm_bank = None
+        keep_warm(warm_bank, HEAD_WARM[0])
         w1_flat = w1_rows[:].rearrange("p r h -> p (r h)")
         w1_grouped = grouped_tile("a_grouped")
         for h in range(HALVES):
@@ -288,20 +298,23 @@ def tile_brainfunctionalconnectivityfeatureextrac_pa_v_kernel(
             nc.vector.tensor_copy(out=sorted_view(dst[:]), in_=by_run(w1_flat[:, h * HALF : (h + 1) * HALF]))
         for h in range(HALVES):
             copy_tiles_apart(w1_grouped, h, transpose_sorted(("w1", h)))
+        keep_warm(warm_bank, HEAD_WARM[1])
         mask_grad(0, 0)
-        mask_grad(0, 1)
+        grad_to_features(0, 0)
+        keep_warm(warm_bank, HEAD_WARM[2])
         w1_mx = mx_pair(keep, "w1", "w1", 1)
         quantize(w1_mx, E4M3, w1_grouped)
+        mask_grad(0, 1)
+        grad_to_features(0, 1)
         neg_d = keep.tile([P, T], F32, name="neg_d")
         nc.vector.tensor_scalar(out=neg_d[:], in0=d_by4[:], scalar1=-1.0, scalar2=None, op0=ALU.mult)
-        grad_to_features(0, 0)
-        grad_to_features(0, 1)
 
         w_mx = mx_pair(keep, "w", "w", 1)
         w_t = keep.tile([P, T, N], F32, name="w_t")
         mask = keep.tile([P, T, N], BF16, name="mask")
         d_rows = keep.tile([P, T], F32, name="d_rows")
         factor = keep.tile([P, T], F32, name="factor")
+        adj_rows = keep.tile([P, T, N], BF16, name="adj_rows")
         ident_bf = keep.tile([P, P], BF16, name="ident_bf")
         make_identity(nc, ident_bf[:])
 
@@ -315,92 +328,105 @@ def tile_brainfunctionalconnectivityfeatureextrac_pa_v_kernel(
 
         last = B - 1
         g_mx[0] = mx_pair(work, "g", "g", 2)
-        for h in range(HALVES):
+
+        def quantize_first_grad(h):
             cols = slice(h * N // 2, (h + 1) * N // 2)
             nc.vector.quantize_mx(
                 out=g_mx[0][0][:, cols].bitcast(E5M2),
                 scales=g_mx[0][1][:, cols],
                 in_=g_grouped[0][:, h * HALF : (h + 1) * HALF],
             )
-        for k in range(last):
-            if k + 2 < B:
-                load_x(k + 2)
+
+        quantize_first_grad(0)
+        first_product(0, 0)
+        first_product(0, 1)
+        mask_grad(1, 0)
+        quantize_first_grad(1)
+        grad_to_features(1, 0)
+        first_product(0, 2)
+        first_product(0, 3)
+        mask_grad(1, 1)
+        grad_to_features(1, 1)
+        keep_warm(warm_bank, HEAD_WARM[3])
+        x_to_channels(0, 0)
+        x_to_channels(0, 1)
+        scale_rows(0, 0)
+        scale_rows(0, 1)
+        transpose_dz1(0, 0)
+        transpose_dz1(0, 1)
+        quantize_grad(1)
+        w_grouped = grouped_tile("a_grouped")
+        nc.vector.tensor_scalar(
+            out=w_grouped[:].rearrange("p (s m t) -> p s m t", s=T, t=T),
+            in0=adj_by4[:].rearrange("p (t m s) -> p s m t", s=T, t=T),
+            scalar1=bias[:],
+            scalar2=0.0,
+            op0=ALU.add,
+            op1=ALU.max,
+        )
+        mask_grad(2, 0)
+        load_gz(3)
+
+        for k in range(1, last):
+            load_x(k + 1)
             if k + 3 < B:
                 load_gz(k + 3)
+            if k == 1:
+                nc.sync.dma_start(out=adj_rows[:], in_=adj.rearrange("(r p) j -> p r j", p=P))
             if k == 2:
                 with nc.allow_non_contiguous_dma(reason="one factor for each row"):
                     nc.sync.dma_start(out=d_rows[:], in_=d.rearrange("(r p) -> p r", p=P))
-            if k >= 1:
-                copy_dz1_t(k - 1, 0)
-                copy_dz1_t(k - 1, 1)
+            if k >= 2:
+                quantize_dz1(k - 2)
+            if k >= 3:
+                finish_dx(k - 3, 3)
+            copy_dz1_t(k - 1, 0)
+            copy_dz1_t(k - 1, 1)
             first_product(k, 0)
             first_product(k, 1)
-            mask_grad(k + 1, 0)
+            if k >= 2:
+                mix_nodes(k - 2, 0)
             grad_to_features(k + 1, 0)
-            if k >= 1:
-                quantize_x_t(k)
-                quantize_dz1_t(k - 1)
             first_product(k, 2)
+            if k >= 2:
+                mix_nodes(k - 2, 1)
             first_product(k, 3)
+            quantize_x_t(k - 1)
+            mask_grad(k + 1, 1)
+            quantize_dz1_t(k - 1)
+            interleave_on_scalar(k - 1, 0)
+            grad_to_features(k + 1, 1, WARM[0])
+            interleave_on_scalar(k - 1, 1)
+            x_to_channels(k, 0)
             if k >= 2:
                 finish_dx(k - 2, 0)
                 mix_nodes(k - 2, 2)
+            else:
+                quantize(w_mx, E4M3, w_grouped)
+            p_pass(0, k - 1)
+            x_to_channels(k, 1)
             scale_rows(k, 0)
             if k >= 2:
                 finish_dx(k - 2, 1)
                 mix_nodes(k - 2, 3)
-            if k == 0:
-                w_grouped = grouped_tile("a_grouped")
-                nc.vector.tensor_scalar(
-                    out=w_grouped[:].rearrange("p (s m t) -> p s m t", s=T, t=T),
-                    in0=adj_by4[:].rearrange("p (t m s) -> p s m t", s=T, t=T),
-                    scalar1=bias[:],
-                    scalar2=0.0,
-                    op0=ALU.add,
-                    op1=ALU.max,
-                )
-                x_to_channels(0, 0)
-                x_to_channels(0, 1)
-            else:
-                interleave_on_scalar(k - 1, 0)
-                interleave_on_scalar(k - 1, 1)
-            mask_grad(k + 1, 1)
             scale_rows(k, 1)
-            if k >= 1:
-                interleave_on_vector(k - 1)
-            grad_to_features(k + 1, 1)
-            x_to_channels(k + 1, 0)
-            if k >= 1:
-                p_pass(0, k - 1)
-                p_pass(1, k - 1)
-            x_to_channels(k + 1, 1)
             transpose_dz1(k, 0)
-            transpose_dz1(k, 1)
+            transpose_dz1(k, 1, WARM[1])
+            p_pass(1, k - 1)
+            interleave_on_vector(k - 1)
             if k >= 2:
                 finish_dx(k - 2, 2)
-                finish_dx(k - 2, 3)
-            if k == 1:
-                nc.vector.tensor_scalar(
-                    out=mask[:], in0=adj_rows[:], scalar1=bias[:], scalar2=0.0, op0=ALU.add, op1=ALU.is_gt
-                )
-            if k == 3:
-                nc.vector.scalar_tensor_tensor(
-                    out=factor[:], in0=d_rows[:], scalar=-0.5, in1=d_rows[:], op0=ALU.mult, op1=ALU.mult
-                )
-            if k >= 1:
-                quantize_dz1(k - 1)
-                mix_nodes(k - 1, 0)
-                mix_nodes(k - 1, 1)
-            else:
-                quantize(w_mx, E4M3, w_grouped)
-                quantize_x_t(0)
+            if k + 2 < B:
+                mask_grad(k + 2, 0, (0,))
             quantize_grad(k + 1)
+            if k + 2 < B:
+                mask_grad(k + 2, 0, (1,))
 
         col_sums = keep.tile([P, T], F32, name="col_sums")
         row_sums = keep.tile([P, T], F32, name="row_sums")
         both_sums = keep.tile([P, T], F32, name="both_sums")
         shift = keep.tile([P, T], F32, name="shift")
-        p_d = keep.tile([P, T, N], F32, name="p_d")
+        p_d = work.tile([P, T, N], F32, name="p_d", tag="rows_f32", bufs=5)
         p_wd = keep.tile([P, T, N], F32, name="p_wd")
         pd_banks = {}
 
@@ -429,80 +455,94 @@ def tile_brainfunctionalconnectivityfeatureextrac_pa_v_kernel(
             for s in range(T):
                 nc.tensor.transpose(pd_banks[r][:, s, :], p_d[:, s, r * P : (r + 1) * P], ident[:])
 
+        nc.vector.tensor_scalar(
+            out=mask[:], in0=adj_rows[:], scalar1=bias[:], scalar2=0.0, op0=ALU.add, op1=ALU.is_gt
+        )
+        quantize_dz1(last - 2)
+        finish_dx(last - 3, 3)
         copy_dz1_t(last - 1, 0)
         copy_dz1_t(last - 1, 1)
         first_product(last, 0)
         first_product(last, 1)
-        finish_dx(last - 2, 0)
-        quantize_x_t(last)
-        finish_dx(last - 2, 1)
-        quantize_dz1_t(last - 1)
+        mix_nodes(last - 2, 0)
         first_product(last, 2)
+        mix_nodes(last - 2, 1)
         first_product(last, 3)
-        mix_nodes(last - 2, 2)
-        mix_nodes(last - 2, 3)
-        transpose_w(0)
-        transpose_w(1)
+        x_to_channels(last, 0)
+        x_to_channels(last, 1)
+        quantize_x_t(last - 1)
+        nc.vector.scalar_tensor_tensor(
+            out=factor[:], in0=d_rows[:], scalar=-0.5, in1=d_rows[:], op0=ALU.mult, op1=ALU.mult
+        )
+        finish_dx(last - 2, 0)
+        quantize_dz1_t(last - 1)
         scale_rows(last, 0)
         transpose_dz1(last, 0)
+        mix_nodes(last - 2, 2)
         p_pass(0, last - 1)
-        p_pass(1, last - 1)
-        finish_dx(last - 2, 2)
+        finish_dx(last - 2, 1)
         scale_rows(last, 1)
         transpose_dz1(last, 1)
-        finish_dx(last - 2, 3)
+        mix_nodes(last - 2, 3)
+        p_pass(1, last - 1)
         copy_dz1_t(last, 0)
         copy_dz1_t(last, 1)
         interleave_on_scalar(last - 1, 0)
         interleave_on_scalar(last - 1, 1)
         interleave_on_vector(last - 1)
-        for b in range(last):
+        finish_dx(last - 2, 2)
+        quantize_x_t(last)
+        finish_dx(last - 2, 3)
+        transpose_w(0)
+        transpose_w(1)
+        for b in range(EARLY_PASSES):
             p_pass(2, b)
-        transpose_w(2)
-        transpose_w(3)
         quantize_dz1_t(last)
         p_pass(0, last)
         p_pass(1, last)
-        p_pass(2, last)
         quantize_dz1(last - 1)
         mix_nodes(last - 1, 0)
         mix_nodes(last - 1, 1)
-        for b in range(B):
-            p_pass(3, b)
+        for b in range(EARLY_PASSES, B):
+            p_pass(2, b)
         interleave_on_scalar(last, 0)
         interleave_on_scalar(last, 1)
+        transpose_w(2)
+        transpose_w(3)
         weigh_p(0)
         weigh_p(1)
-        row_parts = bank("row_parts", [P, T, T, 2])
         finish_dx(last - 1, 0)
+        for b in range(EARLY_PASSES):
+            p_pass(3, b)
         mix_nodes(last - 1, 2)
         finish_dx(last - 1, 1)
+        for b in range(EARLY_PASSES, B):
+            p_pass(3, b)
         mix_nodes(last - 1, 3)
+        row_parts = bank("row_parts", [P, T, T, 2])
         sum_rows(0)
         sum_rows(1)
         weigh_p(2)
         sum_rows(2)
+        finish_dx(last - 1, 2)
         weigh_p(3)
         sum_rows(3)
         for s in range(T):
             scale_p(s)
         interleave_on_vector(last)
-        finish_dx(last - 1, 2)
-        finish_dx(last - 1, 3)
         quantize_dz1(last)
         mix_nodes(last, 0)
+        finish_dx(last - 1, 3)
         mix_nodes(last, 1)
         nc.vector.tensor_reduce(out=row_sums[:], in_=row_parts[:, :, :, 0], axis=mybir.AxisListType.X, op=ALU.add)
+        for r in range(T):
+            transpose_back(r)
         finish_dx(last, 0)
         mix_nodes(last, 2)
         nc.vector.tensor_tensor(out=both_sums[:], in0=col_sums[:], in1=row_sums[:], op=ALU.add)
         finish_dx(last, 1)
         mix_nodes(last, 3)
-        for r in range(T):
-            transpose_back(r)
         nc.vector.tensor_tensor(out=shift[:], in0=both_sums[:], in1=factor[:], op=ALU.mult)
-        finish_dx(last, 2)
-        finish_dx(last, 3)
         for r in range(T):
             nc.vector.scalar_tensor_tensor(
                 out=p_wd[:, r, :],
@@ -513,3 +553,6 @@ def tile_brainfunctionalconnectivityfeatureextrac_pa_v_kernel(
                 op1=ALU.mult,
             )
             nc.sync.dma_start(out=out_1[r * P : (r + 1) * P, :], in_=p_wd[:, r, :])
+            if r == 0:
+                finish_dx(last, 2)
+                finish_dx(last, 3)

@@ -26,7 +26,7 @@ EARLY_PASSES = 5
 WARM = (0, 0)
 HEAD_WARM = (0, 0, 0, 0)
 SCALE_ENGINE = "vvvv"
-VECTOR_SHARE = (64, 0, 0, 0, 0, 0, 64, 0)
+VECTOR_SHARE = (64, 40, 40, 40, 40, 40, 64, 0)
 
 
 def tile_brainfunctionalconnectivityfeatureextrac_pa_v_kernel(
@@ -69,10 +69,11 @@ def tile_brainfunctionalconnectivityfeatureextrac_pa_v_kernel(
         def grouped_tile(tag):
             return work.tile([P, N * T], BF16, name=tag, tag=tag, bufs=2, align_bytes=64)
 
+        ident_bf = keep.tile([P, P], BF16, name="ident_bf")
+        make_identity(nc, ident_bf[:])
+        zeros = None
         ident = keep.tile([P, P], F32, name="ident")
         make_identity(nc, ident[:])
-        ones = keep.tile([P, 2], F32, name="ones")
-        nc.gpsimd.memset(ones[:], 1.0)
 
         g_half, z_half, x_rows = {}, {}, {}
         sorted_half, g_grouped, g_mx = {}, {}, {}
@@ -116,7 +117,9 @@ def tile_brainfunctionalconnectivityfeatureextrac_pa_v_kernel(
 
         def keep_warm(acc, count):
             for n in range(count):
-                nc.tensor.matmul(out=acc[:, 0, :], lhsT=ident[:], rhs=ident[:], start=True, stop=True)
+                nc.tensor.matmul(
+                    out=acc[:].rearrange("p s m -> p (s m)"), lhsT=ident_bf[:], rhs=zeros[:], start=True, stop=True
+                )
 
         def transpose_sorted(key, warm=0):
             words = sorted_half[key][:].bitcast(F32)
@@ -177,18 +180,24 @@ def tile_brainfunctionalconnectivityfeatureextrac_pa_v_kernel(
                     func=ACT.Copy,
                     scale=neg_d[:, t : t + 1],
                 )
-            if scale_engine(b, t) == "g":
+
+        def scale_engine(b, t):
+            return SCALE_ENGINE[t]
+
+        def scale_rows_on_gpsimd(b, h):
+            pair = work.tile([P, 2], F32, name="neg_pair", tag="neg_pair", bufs=2)
+            nc.vector.tensor_scalar(
+                out=pair[:], in0=d_by4[:, 2 * h : 2 * h + 2], scalar1=-1.0, scalar2=None, op0=ALU.mult
+            )
+            for t in (2 * h, 2 * h + 1):
                 nc.gpsimd.tensor_scalar(
-                    out=dst,
+                    out=dz1[b][:, tile_cols(t)].rearrange("p (u w e) -> p u w e", u=2, e=2),
                     in0=dt1[b][:, tile_cols(t)].rearrange("p (w u e) -> p u w e", u=2, e=2),
-                    scalar1=neg_d[:, t : t + 1],
+                    scalar1=pair[:, t % 2 : t % 2 + 1],
                     scalar2=0.0,
                     op0=ALU.mult,
                     op1=ALU.add,
                 )
-
-        def scale_engine(b, t):
-            return SCALE_ENGINE[t]
 
         def scale_rows(b, h):
             for t in (2 * h, 2 * h + 1):
@@ -315,8 +324,6 @@ def tile_brainfunctionalconnectivityfeatureextrac_pa_v_kernel(
         d_rows = keep.tile([P, T], F32, name="d_rows")
         factor = keep.tile([P, T], F32, name="factor")
         adj_rows = keep.tile([P, T, N], BF16, name="adj_rows")
-        ident_bf = keep.tile([P, P], BF16, name="ident_bf")
-        make_identity(nc, ident_bf[:])
 
         def transpose_w(s):
             acc = psum.tile([P, T, P], BF16, name="adj_t", tag="scalar_side", bufs=6 - P_IN_LOOP)
@@ -378,8 +385,6 @@ def tile_brainfunctionalconnectivityfeatureextrac_pa_v_kernel(
                     nc.sync.dma_start(out=d_rows[:], in_=d.rearrange("(r p) -> p r", p=P))
             if k >= 2:
                 quantize_dz1(k - 2)
-            if k >= 3:
-                finish_dx(k - 3, 3)
             copy_dz1_t(k - 1, 0)
             copy_dz1_t(k - 1, 1)
             first_product(k, 0)
@@ -393,6 +398,8 @@ def tile_brainfunctionalconnectivityfeatureextrac_pa_v_kernel(
             first_product(k, 3)
             quantize_x_t(k - 1)
             mask_grad(k + 1, 1)
+            if k >= 2:
+                scale_rows_on_gpsimd(k, 0)
             quantize_dz1_t(k - 1)
             interleave_on_scalar(k - 1, 0)
             grad_to_features(k + 1, 1, WARM[0])
@@ -400,24 +407,31 @@ def tile_brainfunctionalconnectivityfeatureextrac_pa_v_kernel(
             x_to_channels(k, 0)
             if k >= 2:
                 finish_dx(k - 2, 0)
+                finish_dx(k - 2, 1)
                 mix_nodes(k - 2, 2)
+                mix_nodes(k - 2, 3)
             else:
                 quantize(w_mx, E4M3, w_grouped)
+                scale_rows(k, 0)
             p_pass(0, k - 1)
             x_to_channels(k, 1)
-            scale_rows(k, 0)
-            if k >= 2:
-                finish_dx(k - 2, 1)
-                mix_nodes(k - 2, 3)
-            scale_rows(k, 1)
-            transpose_dz1(k, 0)
-            transpose_dz1(k, 1, WARM[1])
-            p_pass(1, k - 1)
             interleave_on_vector(k - 1)
             if k >= 2:
-                finish_dx(k - 2, 2)
+                scale_rows_on_gpsimd(k, 1)
+            else:
+                scale_rows(k, 1)
             if k + 2 < B:
                 mask_grad(k + 2, 0, (0,))
+            else:
+                nc.vector.tensor_scalar(
+                    out=mask[:], in0=adj_rows[:], scalar1=bias[:], scalar2=0.0, op0=ALU.add, op1=ALU.is_gt
+                )
+            transpose_dz1(k, 0)
+            p_pass(1, k - 1)
+            transpose_dz1(k, 1, WARM[1])
+            if k >= 2:
+                finish_dx(k - 2, 2)
+                finish_dx(k - 2, 3)
             quantize_grad(k + 1)
             if k + 2 < B:
                 mask_grad(k + 2, 0, (1,))
@@ -428,6 +442,7 @@ def tile_brainfunctionalconnectivityfeatureextrac_pa_v_kernel(
         shift = keep.tile([P, T], F32, name="shift")
         p_d = work.tile([P, T, N], F32, name="p_d", tag="rows_f32", bufs=5)
         p_wd = keep.tile([P, T, N], F32, name="p_wd")
+        unused = keep.tile([P, P], F32, name="unused")
         pd_banks = {}
 
         def scale_p(s):
@@ -444,22 +459,26 @@ def tile_brainfunctionalconnectivityfeatureextrac_pa_v_kernel(
                 accum_out=col_sums[:, s : s + 1],
             )
 
-        def sum_rows(s):
+        def sum_rows():
+            parts = bank("row_parts", [P, T, P])
             for r in range(T):
-                nc.tensor.matmul(
-                    out=row_parts[:, r, s, :], lhsT=p_wd[:, s, r * P : (r + 1) * P], rhs=ones[:], start=True, stop=True
-                )
+                for s in range(T):
+                    nc.tensor.matmul(
+                        out=parts[:, r, :],
+                        lhsT=p_wd[:, s, r * P : (r + 1) * P],
+                        rhs=ident[:],
+                        start=s == 0,
+                        stop=s == T - 1,
+                        is_transpose=True,
+                    )
+            return parts
 
         def transpose_back(r):
             pd_banks[r] = held_bank("pd_held", [P, T, P]) if r < P_IN_LOOP else bank("pd_acc", [P, T, P])
             for s in range(T):
                 nc.tensor.transpose(pd_banks[r][:, s, :], p_d[:, s, r * P : (r + 1) * P], ident[:])
 
-        nc.vector.tensor_scalar(
-            out=mask[:], in0=adj_rows[:], scalar1=bias[:], scalar2=0.0, op0=ALU.add, op1=ALU.is_gt
-        )
         quantize_dz1(last - 2)
-        finish_dx(last - 3, 3)
         copy_dz1_t(last - 1, 0)
         copy_dz1_t(last - 1, 1)
         first_product(last, 0)
@@ -495,6 +514,7 @@ def tile_brainfunctionalconnectivityfeatureextrac_pa_v_kernel(
         finish_dx(last - 2, 3)
         transpose_w(0)
         transpose_w(1)
+        transpose_w(2)
         for b in range(EARLY_PASSES):
             p_pass(2, b)
         quantize_dz1_t(last)
@@ -502,47 +522,48 @@ def tile_brainfunctionalconnectivityfeatureextrac_pa_v_kernel(
         p_pass(1, last)
         quantize_dz1(last - 1)
         mix_nodes(last - 1, 0)
-        mix_nodes(last - 1, 1)
         for b in range(EARLY_PASSES, B):
             p_pass(2, b)
+        mix_nodes(last - 1, 1)
         interleave_on_scalar(last, 0)
-        interleave_on_scalar(last, 1)
-        transpose_w(2)
         transpose_w(3)
+        interleave_on_scalar(last, 1)
         weigh_p(0)
         weigh_p(1)
         finish_dx(last - 1, 0)
         for b in range(EARLY_PASSES):
             p_pass(3, b)
         mix_nodes(last - 1, 2)
+        weigh_p(2)
         finish_dx(last - 1, 1)
         for b in range(EARLY_PASSES, B):
             p_pass(3, b)
         mix_nodes(last - 1, 3)
-        row_parts = bank("row_parts", [P, T, T, 2])
-        sum_rows(0)
-        sum_rows(1)
-        weigh_p(2)
-        sum_rows(2)
         finish_dx(last - 1, 2)
-        weigh_p(3)
-        sum_rows(3)
-        for s in range(T):
-            scale_p(s)
-        interleave_on_vector(last)
         quantize_dz1(last)
         mix_nodes(last, 0)
+        weigh_p(3)
+        for s in range(T):
+            scale_p(s)
+        row_parts = sum_rows()
+        for r in range(T):
+            nc.scalar.activation(
+                out=unused[:], in_=row_parts[:, r, :], func=ACT.Copy, accum_out=row_sums[:, r : r + 1]
+            )
         finish_dx(last - 1, 3)
         mix_nodes(last, 1)
-        nc.vector.tensor_reduce(out=row_sums[:], in_=row_parts[:, :, :, 0], axis=mybir.AxisListType.X, op=ALU.add)
-        for r in range(T):
-            transpose_back(r)
+        transpose_back(0)
         finish_dx(last, 0)
         mix_nodes(last, 2)
-        nc.vector.tensor_tensor(out=both_sums[:], in0=col_sums[:], in1=row_sums[:], op=ALU.add)
+        transpose_back(1)
         finish_dx(last, 1)
         mix_nodes(last, 3)
+        transpose_back(2)
+        transpose_back(3)
+        nc.vector.tensor_tensor(out=both_sums[:], in0=col_sums[:], in1=row_sums[:], op=ALU.add)
+        finish_dx(last, 2)
         nc.vector.tensor_tensor(out=shift[:], in0=both_sums[:], in1=factor[:], op=ALU.mult)
+        finish_dx(last, 3)
         for r in range(T):
             nc.vector.scalar_tensor_tensor(
                 out=p_wd[:, r, :],
@@ -553,6 +574,3 @@ def tile_brainfunctionalconnectivityfeatureextrac_pa_v_kernel(
                 op1=ALU.mult,
             )
             nc.sync.dma_start(out=out_1[r * P : (r + 1) * P, :], in_=p_wd[:, r, :])
-            if r == 0:
-                finish_dx(last, 2)
-                finish_dx(last, 3)

@@ -3,11 +3,12 @@ from contextlib import ExitStack
 import concourse.mybir as mybir
 from concourse.masks import make_identity
 
-B, N = 8, 512
+B = 8
+N = 512
 P = 128
 T = 4
-HALVES = 2
-HALF = N * T // HALVES
+HALF = 2 * N
+RUN = 16
 
 FLOPS = 3 * 2 * B * N * N * N
 BYTES = B * N * N * (2 + 2 + 4 + 4) + N * N * (2 + 2 + 4) + N * 4 + 2
@@ -21,18 +22,20 @@ E5M2 = mybir.dt.float8_e5m2_x4
 ALU = mybir.AluOpType
 ACT = mybir.ActivationFunctionType
 
-P_IN_LOOP = 2
-EARLY_PASSES = 5
-WARM = (0, 0)
-HEAD_WARM = (0, 0, 0, 0)
-SCALE_ENGINE = "vvvv"
-VECTOR_SHARE = (64, 40, 40, 40, 40, 40, 64, 0)
+HELD_BANKS, U_BANKS, RING_BANKS = 2, 2, 4
+
+STEADY_SHARE, EDGE_SHARE = 16, 64
+
+EARLY_PASSES = 4
+
+WARM_START, WARM_FILL, WARM_STEP = 5, 3, 1
 
 
 def tile_brainfunctionalconnectivityfeatureextrac_pa_v_kernel(
     tc, x, adj, adj_bias, cheb_w, brelu_bias, z, d, grad_out, out_0, out_1
 ):
     nc = tc.nc
+    last = B - 1
     with ExitStack() as ctx:
         keep = ctx.enter_context(tc.tile_pool(name="keep", bufs=1))
         load = ctx.enter_context(tc.tile_pool(name="load", bufs=3))
@@ -40,24 +43,30 @@ def tile_brainfunctionalconnectivityfeatureextrac_pa_v_kernel(
         psum = ctx.enter_context(tc.psum_pool(name="psum", bufs=1))
         ctx.enter_context(tc.manual_schedule())
 
-        def bank(name, shape):
-            return psum.tile(shape, F32, name=name, tag="scalar_side", bufs=6 - P_IN_LOOP)
+        def ring_bank(name, shape, dtype=F32):
+            return psum.tile(shape, dtype, name=name, tag="ring", bufs=RING_BANKS)
 
         def held_bank(name, shape):
-            return psum.tile(shape, F32, name=name, tag="p_held", bufs=P_IN_LOOP)
+            return psum.tile(shape, F32, name=name, tag="held", bufs=HELD_BANKS)
 
-        def mx_pair(pool, name, tag, bufs):
-            codes = pool.tile([P, N], U32, name=name + "_codes", tag=tag + "_codes", bufs=bufs, align_bytes=64)
-            scales = pool.tile([P, N], U8, name=name + "_scales", tag=tag + "_scales", bufs=bufs, align_bytes=64)
+        def rows_f32(name, shape):
+            return work.tile(shape, F32, name=name, tag="rows_f32", bufs=5)
+
+        def grouped_tile(tag):
+            return work.tile([P, N * T], BF16, name=tag, tag=tag, bufs=2, align_bytes=64)
+
+        def mx_operand(pool, tag, bufs):
+            codes = pool.tile([P, N], U32, name=tag + "_codes", tag=tag + "_codes", bufs=bufs, align_bytes=64)
+            scales = pool.tile([P, N], U8, name=tag + "_scales", tag=tag + "_scales", bufs=bufs, align_bytes=64)
             return codes, scales
 
-        def quantize(pair, fmt, grouped):
-            nc.vector.quantize_mx(out=pair[0][:].bitcast(fmt), scales=pair[1][:], in_=grouped[:])
+        def quantize(operand, fmt, grouped):
+            nc.vector.quantize_mx(out=operand[0][:].bitcast(fmt), scales=operand[1][:], in_=grouped[:])
 
-        def mx_pass(acc, lhs, lhs_fmt, tile_index, rhs, rhs_fmt, start, stop):
-            cols = slice(tile_index * P, (tile_index + 1) * P)
+        def mx_pass(acc, lhs, lhs_fmt, row_tile, rhs, rhs_fmt, start, stop):
+            cols = slice(row_tile * P, (row_tile + 1) * P)
             nc.tensor.matmul_mx(
-                out=acc,
+                out=acc[:],
                 lhsT=lhs[0][:, cols].bitcast(lhs_fmt),
                 lhsT_scale=lhs[1][:, cols],
                 rhs=rhs[0][:].bitcast(rhs_fmt),
@@ -66,23 +75,30 @@ def tile_brainfunctionalconnectivityfeatureextrac_pa_v_kernel(
                 stop=stop,
             )
 
-        def grouped_tile(tag):
-            return work.tile([P, N * T], BF16, name=tag, tag=tag, bufs=2, align_bytes=64)
+        def tile_cols(t):
+            return slice(t * N, (t + 1) * N)
 
         ident_bf = keep.tile([P, P], BF16, name="ident_bf")
         make_identity(nc, ident_bf[:])
-        zeros = None
+        zeros = keep.tile([P, N], BF16, name="zeros")
+        nc.gpsimd.memset(zeros[:], 0.0)
         ident = keep.tile([P, P], F32, name="ident")
         make_identity(nc, ident[:])
 
-        g_half, z_half, x_rows = {}, {}, {}
-        sorted_half, g_grouped, g_mx = {}, {}, {}
-        dt1, dz1, z_banks = {}, {}, {}
-        zt_grouped, xt_grouped, zt_mx, xt_mx = {}, {}, {}, {}
-        a_grouped, a_mx, u_banks, p_banks = {}, {}, {}, {}
+        def keep_warm(acc, count):
+            for n in range(count):
+                nc.tensor.matmul(
+                    out=acc[:].rearrange("p s m -> p (s m)"), lhsT=ident_bf[:], rhs=zeros[:], start=True, stop=True
+                )
+
+        g_half, z_half, x_rows, sorted_half = {}, {}, {}, {}
+        g_grouped, zt_grouped, xt_grouped, a_grouped = {}, {}, {}, {}
+        g_mx, zt_mx, xt_mx, a_mx = {}, {}, {}, {}
+        dt1, dz1, z_banks, u_banks, p_banks, pd_banks = {}, {}, {}, {}, {}, {}
+
 
         def load_gz(b):
-            for h in range(HALVES):
+            for h in range(2):
                 cols = slice(h * HALF, (h + 1) * HALF)
                 g_half[b, h] = load.tile([P, HALF], BF16, name="g_half", tag="g_half", bufs=6)
                 nc.sync.dma_start(out=g_half[b, h][:], in_=grad_out[b].rearrange("(p t) h -> p (t h)", t=T)[:, cols])
@@ -93,174 +109,161 @@ def tile_brainfunctionalconnectivityfeatureextrac_pa_v_kernel(
             x_rows[b] = load.tile([P, N * T], BF16, name="x_rows", tag="x_rows", bufs=3)
             nc.sync.dma_start(out=x_rows[b][:], in_=x[b].rearrange("(p t) c -> p (t c)", t=T))
 
-        def by_run(ap):
-            return ap.rearrange("p (a u r) -> p u a r", u=2, r=16)
+
+        def unsorted_view(ap):
+            return ap.rearrange("p (a u r) -> p u a r", u=2, r=RUN)
 
         def sorted_view(ap):
-            return ap.rearrange("p (u a r) -> p u a r", u=2, r=16)
+            return ap.rearrange("p (u a r) -> p u a r", u=2, r=RUN)
 
         def new_sorted_half(key):
             sorted_half[key] = work.tile([P, HALF], BF16, name="sorted_half", tag="sorted_half", bufs=4)
-            return sorted_half[key]
 
         def mask_grad(b, h, parts=(0, 1)):
-            dst = new_sorted_half((b, h)) if 0 in parts else sorted_half[b, h]
             for u in parts:
+                if u == 0:
+                    new_sorted_half((b, h))
                 nc.vector.scalar_tensor_tensor(
-                    out=sorted_view(dst[:])[:, u],
-                    in0=by_run(z_half[b, h][:])[:, u],
+                    out=sorted_view(sorted_half[b, h][:])[:, u],
+                    in0=unsorted_view(z_half[b, h][:])[:, u],
                     scalar=0.0,
-                    in1=by_run(g_half[b, h][:])[:, u],
+                    in1=unsorted_view(g_half[b, h][:])[:, u],
                     op0=ALU.is_gt,
                     op1=ALU.mult,
                 )
 
-        def keep_warm(acc, count):
-            for n in range(count):
-                nc.tensor.matmul(
-                    out=acc[:].rearrange("p s m -> p (s m)"), lhsT=ident_bf[:], rhs=zeros[:], start=True, stop=True
-                )
-
-        def transpose_sorted(key, warm=0):
+        def sorted_to_grouped(key, grouped, h, warm=0):
             words = sorted_half[key][:].bitcast(F32)
-            acc = bank("sorted_t", [P, 4, P])
+            acc = ring_bank("sorted_t", [P, 4, P])
             keep_warm(acc, warm)
             for t in range(2):
                 for u in range(2):
                     first = (2 * u + t) * P
                     nc.tensor.transpose(acc[:, 2 * t + u, :], words[:, first : first + P], ident[:])
-            return acc
-
-        def copy_tiles_apart(grouped, h, acc):
-            words = grouped[:].bitcast(F32)[:, h * N : (h + 1) * N]
             nc.scalar.copy(
-                out=words.rearrange("q (t p u) -> q t p u", t=2, u=2),
+                out=grouped[:].bitcast(F32)[:, tile_cols(h)].rearrange("q (t p u) -> q t p u", t=2, u=2),
                 in_=acc[:].rearrange("q (t u) p -> q t p u", u=2),
             )
 
-        def transpose_rows(rows, h, warm=0):
-            words = rows[:].bitcast(F32)
-            acc = bank("rows_t", [P, 4, P])
-            keep_warm(acc, warm)
-            for t in range(2):
-                for u in range(2):
-                    first = (2 * h + t) * 2 * P
-                    nc.tensor.transpose(acc[:, 2 * t + u, :], words[:, first + u : first + 2 * P : 2], ident[:])
-            return acc
-
-        def copy_rows_in_order(grouped, h, acc):
-            words = grouped[:].bitcast(F32).rearrange("q (p h s) -> q h p s", h=2, s=4)
-            nc.scalar.copy(out=words[:, h], in_=acc[:].rearrange("q s p -> q p s"))
-
         def grad_to_features(b, h, warm=0):
-            acc = transpose_sorted((b, h), warm)
             if h == 0:
                 g_grouped[b] = grouped_tile("g_grouped")
-            copy_tiles_apart(g_grouped[b], h, acc)
+            sorted_to_grouped((b, h), g_grouped[b], h, warm)
 
         def quantize_grad(b):
-            g_mx[b] = mx_pair(work, "g", "g", 2)
+            g_mx[b] = mx_operand(work, "g", 2)
             quantize(g_mx[b], E5M2, g_grouped[b])
 
-        def tile_cols(t):
-            return slice(t * N, (t + 1) * N)
+        def quantize_first_grad(h):
+            if h == 0:
+                g_mx[0] = mx_operand(work, "g", 2)
+            cols = slice(h * 2 * P, (h + 1) * 2 * P)
+            nc.vector.quantize_mx(
+                out=g_mx[0][0][:, cols].bitcast(E5M2),
+                scales=g_mx[0][1][:, cols],
+                in_=g_grouped[0][:, h * HALF : (h + 1) * HALF],
+            )
+
 
         def first_product(b, t):
             if t == 0:
-                dt1[b] = work.tile([P, T * N], F32, name="rows_f32", tag="rows_f32", bufs=5)
+                dt1[b] = rows_f32("dt1", [P, T * N])
                 dz1[b] = work.tile([P, T * N], BF16, name="dz1", tag="dz1", bufs=3)
-            acc = bank("dt1_acc", [P, N])
-            mx_pass(acc[:], g_mx[b], E5M2, t, w1_mx, E4M3, True, True)
+            acc = ring_bank("dt1_acc", [P, N])
+            mx_pass(acc, g_mx[b], E5M2, t, w1_mx, E4M3, True, True)
             nc.scalar.copy(out=dt1[b][:, tile_cols(t)], in_=acc[:])
+
+        def scale_views(b, t):
             dst = dz1[b][:, tile_cols(t)].rearrange("p (u w e) -> p u w e", u=2, e=2)
-            if scale_engine(b, t) == "s":
-                nc.scalar.activation(
-                    out=dst,
-                    in_=acc[:].rearrange("p (w u e) -> p u w e", u=2, e=2),
-                    func=ACT.Copy,
-                    scale=neg_d[:, t : t + 1],
-                )
+            src = dt1[b][:, tile_cols(t)].rearrange("p (w u e) -> p u w e", u=2, e=2)
+            return dst, src
 
-        def scale_engine(b, t):
-            return SCALE_ENGINE[t]
+        def scale_on_vector(b, tiles):
+            for t in tiles:
+                dst, src = scale_views(b, t)
+                nc.vector.tensor_scalar(out=dst, in0=src, scalar1=neg_d[:, t : t + 1], scalar2=None, op0=ALU.mult)
 
-        def scale_rows_on_gpsimd(b, h):
-            pair = work.tile([P, 2], F32, name="neg_pair", tag="neg_pair", bufs=2)
-            nc.vector.tensor_scalar(
-                out=pair[:], in0=d_by4[:, 2 * h : 2 * h + 2], scalar1=-1.0, scalar2=None, op0=ALU.mult
-            )
-            for t in (2 * h, 2 * h + 1):
-                nc.gpsimd.tensor_scalar(
-                    out=dz1[b][:, tile_cols(t)].rearrange("p (u w e) -> p u w e", u=2, e=2),
-                    in0=dt1[b][:, tile_cols(t)].rearrange("p (w u e) -> p u w e", u=2, e=2),
-                    scalar1=pair[:, t % 2 : t % 2 + 1],
-                    scalar2=0.0,
-                    op0=ALU.mult,
-                    op1=ALU.add,
-                )
 
-        def scale_rows(b, h):
-            for t in (2 * h, 2 * h + 1):
-                if scale_engine(b, t) == "v":
-                    nc.vector.tensor_scalar(
-                        out=dz1[b][:, tile_cols(t)].rearrange("p (u w e) -> p u w e", u=2, e=2),
-                        in0=dt1[b][:, tile_cols(t)].rearrange("p (w u e) -> p u w e", u=2, e=2),
-                        scalar1=neg_d[:, t : t + 1],
-                        scalar2=None,
-                        op0=ALU.mult,
-                    )
+        def factor_for_gpsimd(t):
+            neg_column = work.tile([P, 1], F32, name="neg_column", tag="neg_column", bufs=2)
+            nc.vector.tensor_scalar(out=neg_column[:], in0=d_by4[:, t : t + 1], scalar1=-1.0, scalar2=None, op0=ALU.mult)
+            return neg_column
+
+        def scale_on_gpsimd(b, t, neg_column):
+            dst, src = scale_views(b, t)
+            nc.gpsimd.tensor_scalar(out=dst, in0=src, scalar1=neg_column[:], scalar2=0.0, op0=ALU.mult, op1=ALU.add)
+
+
+        def copy_nodes_in_order(grouped, h, acc):
+            words = grouped[:].bitcast(F32).rearrange("q (p h s) -> q h p s", h=2, s=4)
+            nc.scalar.copy(out=words[:, h], in_=acc[:].rearrange("q s p -> q p s"))
 
         def transpose_dz1(b, h, warm=0):
             words = dz1[b][:].bitcast(F32)
-            z_banks[b, h] = bank("dz1_t", [P, 4, P])
+            z_banks[b, h] = ring_bank("dz1_t", [P, 4, P])
             keep_warm(z_banks[b, h], warm)
             for s in range(4):
                 first = (4 * h + s) * P
                 nc.tensor.transpose(z_banks[b, h][:, s, :], words[:, first : first + P], ident[:])
 
-        def copy_dz1_t(b, h):
-            if h == 0:
-                zt_grouped[b] = grouped_tile("zt_grouped")
-            copy_rows_in_order(zt_grouped[b], h, z_banks[b, h])
+        def copy_dz1_t(b):
+            zt_grouped[b] = grouped_tile("zt_grouped")
+            for h in range(2):
+                copy_nodes_in_order(zt_grouped[b], h, z_banks[b, h])
 
         def quantize_dz1_t(b):
-            zt_mx[b] = mx_pair(keep, "zt", "zt", B)
+            zt_mx[b] = mx_operand(keep, "zt", B)
             quantize(zt_mx[b], E5M2, zt_grouped[b])
 
-        def x_to_channels(b, h, warm=0):
-            acc = transpose_rows(x_rows[b], h, warm)
+        def x_to_channels(b, h):
+            words = x_rows[b][:].bitcast(F32)
+            acc = ring_bank("x_t", [P, 4, P])
+            for t in range(2):
+                for u in range(2):
+                    first = (2 * h + t) * 2 * P
+                    nc.tensor.transpose(acc[:, 2 * t + u, :], words[:, first + u : first + 2 * P : 2], ident[:])
             if h == 0:
                 xt_grouped[b] = grouped_tile("xt_grouped")
-            copy_rows_in_order(xt_grouped[b], h, acc)
+            copy_nodes_in_order(xt_grouped[b], h, acc)
 
         def quantize_x_t(b):
-            xt_mx[b] = mx_pair(keep, "xt", "xt", B)
+            xt_mx[b] = mx_operand(keep, "xt", B)
             quantize(xt_mx[b], E4M3, xt_grouped[b])
 
-        def interleave_views(b, first, last):
-            src = dz1[b][:].rearrange("p (t u w e) -> p u w t e", t=T, u=2, e=2)[:, :, first:last]
-            dst = a_grouped[b][:].rearrange("p (w u e t) -> p u w t e", t=T, u=2, e=2)[:, :, first:last]
+        def p_pass(s, b):
+            if b == 0:
+                p_banks[s] = held_bank("p_held", [P, N]) if s < HELD_BANKS else ring_bank("p_acc", [P, N])
+            mx_pass(p_banks[s], xt_mx[b], E4M3, s, zt_mx[b], E5M2, b == 0, b == last)
+
+
+        def vector_share(b):
+            if b == last:
+                return 0
+            return EDGE_SHARE if b in (0, last - 1) else STEADY_SHARE
+
+        def interleave_views(b, first, end):
+            src = dz1[b][:].rearrange("p (t u w e) -> p u w t e", t=T, u=2, e=2)[:, :, first:end]
+            dst = a_grouped[b][:].rearrange("p (w u e t) -> p u w t e", t=T, u=2, e=2)[:, :, first:end]
             return dst, src
 
         def interleave_on_scalar(b, h):
             if h == 0:
                 a_grouped[b] = grouped_tile("a_grouped")
-            middle = (VECTOR_SHARE[b] + P) // 2
-            dst, src = interleave_views(b, VECTOR_SHARE[b], middle) if h == 0 else interleave_views(b, middle, P)
+            cuts = (vector_share(b), (vector_share(b) + P) // 2, P)
+            dst, src = interleave_views(b, cuts[h], cuts[h + 1])
             nc.scalar.copy(out=dst, in_=src)
 
         def interleave_on_vector(b):
-            if VECTOR_SHARE[b] > 0:
-                dst, src = interleave_views(b, 0, VECTOR_SHARE[b])
-                nc.vector.tensor_copy(out=dst, in_=src)
+            dst, src = interleave_views(b, 0, vector_share(b))
+            nc.vector.tensor_copy(out=dst, in_=src)
 
         def quantize_dz1(b):
-            a_mx[b] = mx_pair(work, "a", "a", 2)
+            a_mx[b] = mx_operand(work, "a", 2)
             quantize(a_mx[b], E5M2, a_grouped[b])
 
         def mix_nodes(b, t):
-            u_banks[b, t] = psum.tile([P, N], F32, name="u_acc", tag="vector_side", bufs=2)
-            mx_pass(u_banks[b, t][:], w_mx, E4M3, t, a_mx[b], E5M2, True, True)
+            u_banks[b, t] = psum.tile([P, N], F32, name="u_acc", tag="u", bufs=U_BANKS)
+            mx_pass(u_banks[b, t], w_mx, E4M3, t, a_mx[b], E5M2, True, True)
 
         def finish_dx(b, t):
             nc.vector.scalar_tensor_tensor(
@@ -271,17 +274,52 @@ def tile_brainfunctionalconnectivityfeatureextrac_pa_v_kernel(
                 op0=ALU.mult,
                 op1=ALU.add,
             )
-            if t % 2 == 1:
-                cols = slice((t - 1) * N, (t + 1) * N)
+            if t % 2 == 1 or b == last:
+                cols = tile_cols(t) if b == last else slice((t - 1) * N, (t + 1) * N)
                 nc.sync.dma_start(out=out_0[b].rearrange("(p t) c -> p (t c)", t=T)[:, cols], in_=dt1[b][:, cols])
 
-        def p_pass(r, b):
-            if b == 0:
-                if r < P_IN_LOOP:
-                    p_banks[r] = held_bank("p_held", [P, N])
-                else:
-                    p_banks[r] = bank("p_acc", [P, N])
-            mx_pass(p_banks[r][:], xt_mx[b], E4M3, r, zt_mx[b], E5M2, b == 0, b == B - 1)
+
+        def transpose_w(s):
+            acc = ring_bank("adj_t", [P, T, P], BF16)
+            for r in range(T):
+                nc.tensor.transpose(acc[:, r, :], adj_rows[:, r, s * P : (s + 1) * P], ident_bf[:])
+            nc.scalar.activation(
+                out=w_t[:, s, :], in_=acc[:].rearrange("p r m -> p (r m)"), func=ACT.Relu, bias=bias[:]
+            )
+
+        def weigh_p(s):
+            nc.vector.scalar_tensor_tensor(
+                out=p_wd[:, s, :],
+                in0=p_banks[s][:],
+                scalar=d_rows[:, s : s + 1],
+                in1=w_t[:, s, :],
+                op0=ALU.mult,
+                op1=ALU.mult,
+                accum_out=col_sums[:, s : s + 1],
+            )
+
+        def scale_p(s):
+            nc.scalar.activation(out=p_d[:, s, :], in_=p_banks[s][:], func=ACT.Copy, scale=d_rows[:, s : s + 1])
+
+        def add_row_tiles():
+            parts = ring_bank("row_parts", [P, T, P])
+            for r in range(T):
+                for s in range(T):
+                    nc.tensor.matmul(
+                        out=parts[:, r, :],
+                        lhsT=p_wd[:, s, r * P : (r + 1) * P],
+                        rhs=ident[:],
+                        start=s == 0,
+                        stop=s == T - 1,
+                        is_transpose=True,
+                    )
+            return parts
+
+        def transpose_back(r):
+            pd_banks[r] = held_bank("pd_held", [P, T, P]) if r < HELD_BANKS else ring_bank("pd_acc", [P, T, P])
+            for s in range(T):
+                nc.tensor.transpose(pd_banks[r][:, s, :], p_d[:, s, r * P : (r + 1) * P], ident[:])
+
 
         w1_rows = keep.tile([P, T, N], BF16, name="w1_rows")
         nc.sync.dma_start(out=w1_rows[:], in_=cheb_w.rearrange("(r p k) h -> k p r h", k=2, p=P)[1])
@@ -298,51 +336,27 @@ def tile_brainfunctionalconnectivityfeatureextrac_pa_v_kernel(
         load_gz(2)
         load_x(1)
 
-        warm_bank = None
-        keep_warm(warm_bank, HEAD_WARM[0])
+        warm_bank = held_bank("warm", [P, 4, P])
+        keep_warm(warm_bank, WARM_START)
         w1_flat = w1_rows[:].rearrange("p r h -> p (r h)")
         w1_grouped = grouped_tile("a_grouped")
-        for h in range(HALVES):
-            dst = new_sorted_half(("w1", h))
-            nc.vector.tensor_copy(out=sorted_view(dst[:]), in_=by_run(w1_flat[:, h * HALF : (h + 1) * HALF]))
-        for h in range(HALVES):
-            copy_tiles_apart(w1_grouped, h, transpose_sorted(("w1", h)))
-        keep_warm(warm_bank, HEAD_WARM[1])
+        for h in range(2):
+            new_sorted_half(("w1", h))
+            nc.vector.tensor_copy(
+                out=sorted_view(sorted_half["w1", h][:]), in_=unsorted_view(w1_flat[:, h * HALF : (h + 1) * HALF])
+            )
+        for h in range(2):
+            sorted_to_grouped(("w1", h), w1_grouped, h)
+        keep_warm(warm_bank, WARM_FILL)
         mask_grad(0, 0)
         grad_to_features(0, 0)
-        keep_warm(warm_bank, HEAD_WARM[2])
-        w1_mx = mx_pair(keep, "w1", "w1", 1)
+        keep_warm(warm_bank, WARM_FILL)
+        w1_mx = mx_operand(keep, "w1", 1)
         quantize(w1_mx, E4M3, w1_grouped)
         mask_grad(0, 1)
         grad_to_features(0, 1)
         neg_d = keep.tile([P, T], F32, name="neg_d")
         nc.vector.tensor_scalar(out=neg_d[:], in0=d_by4[:], scalar1=-1.0, scalar2=None, op0=ALU.mult)
-
-        w_mx = mx_pair(keep, "w", "w", 1)
-        w_t = keep.tile([P, T, N], F32, name="w_t")
-        mask = keep.tile([P, T, N], BF16, name="mask")
-        d_rows = keep.tile([P, T], F32, name="d_rows")
-        factor = keep.tile([P, T], F32, name="factor")
-        adj_rows = keep.tile([P, T, N], BF16, name="adj_rows")
-
-        def transpose_w(s):
-            acc = psum.tile([P, T, P], BF16, name="adj_t", tag="scalar_side", bufs=6 - P_IN_LOOP)
-            for r in range(T):
-                nc.tensor.transpose(acc[:, r, :], adj_rows[:, r, s * P : (s + 1) * P], ident_bf[:])
-            nc.scalar.activation(
-                out=w_t[:, s, :], in_=acc[:].rearrange("p r m -> p (r m)"), func=ACT.Relu, bias=bias[:]
-            )
-
-        last = B - 1
-        g_mx[0] = mx_pair(work, "g", "g", 2)
-
-        def quantize_first_grad(h):
-            cols = slice(h * N // 2, (h + 1) * N // 2)
-            nc.vector.quantize_mx(
-                out=g_mx[0][0][:, cols].bitcast(E5M2),
-                scales=g_mx[0][1][:, cols],
-                in_=g_grouped[0][:, h * HALF : (h + 1) * HALF],
-            )
 
         quantize_first_grad(0)
         first_product(0, 0)
@@ -354,11 +368,10 @@ def tile_brainfunctionalconnectivityfeatureextrac_pa_v_kernel(
         first_product(0, 3)
         mask_grad(1, 1)
         grad_to_features(1, 1)
-        keep_warm(warm_bank, HEAD_WARM[3])
+        keep_warm(warm_bank, WARM_FILL)
         x_to_channels(0, 0)
         x_to_channels(0, 1)
-        scale_rows(0, 0)
-        scale_rows(0, 1)
+        scale_on_vector(0, range(T))
         transpose_dz1(0, 0)
         transpose_dz1(0, 1)
         quantize_grad(1)
@@ -374,7 +387,14 @@ def tile_brainfunctionalconnectivityfeatureextrac_pa_v_kernel(
         mask_grad(2, 0)
         load_gz(3)
 
+        w_mx = mx_operand(keep, "w", 1)
+        adj_rows = keep.tile([P, T, N], BF16, name="adj_rows")
+        d_rows = keep.tile([P, T], F32, name="d_rows")
+        mask = keep.tile([P, T, N], BF16, name="mask")
+
+
         for k in range(1, last):
+            full = k >= 2
             load_x(k + 1)
             if k + 3 < B:
                 load_gz(k + 3)
@@ -383,104 +403,76 @@ def tile_brainfunctionalconnectivityfeatureextrac_pa_v_kernel(
             if k == 2:
                 with nc.allow_non_contiguous_dma(reason="one factor for each row"):
                     nc.sync.dma_start(out=d_rows[:], in_=d.rearrange("(r p) -> p r", p=P))
-            if k >= 2:
+            if full:
                 quantize_dz1(k - 2)
-            copy_dz1_t(k - 1, 0)
-            copy_dz1_t(k - 1, 1)
+            copy_dz1_t(k - 1)
             first_product(k, 0)
             first_product(k, 1)
-            if k >= 2:
+            if full:
                 mix_nodes(k - 2, 0)
             grad_to_features(k + 1, 0)
             first_product(k, 2)
-            if k >= 2:
+            if full:
                 mix_nodes(k - 2, 1)
             first_product(k, 3)
             quantize_x_t(k - 1)
             mask_grad(k + 1, 1)
-            if k >= 2:
-                scale_rows_on_gpsimd(k, 0)
+            if full:
+                neg_column = factor_for_gpsimd(0)
             quantize_dz1_t(k - 1)
+            if full:
+                scale_on_gpsimd(k, 0, neg_column)
             interleave_on_scalar(k - 1, 0)
-            grad_to_features(k + 1, 1, WARM[0])
+            grad_to_features(k + 1, 1, WARM_STEP)
             interleave_on_scalar(k - 1, 1)
             x_to_channels(k, 0)
-            if k >= 2:
+            if full:
                 finish_dx(k - 2, 0)
                 finish_dx(k - 2, 1)
                 mix_nodes(k - 2, 2)
                 mix_nodes(k - 2, 3)
+                scale_on_vector(k, (1,))
             else:
                 quantize(w_mx, E4M3, w_grouped)
-                scale_rows(k, 0)
+                scale_on_vector(k, (0, 1))
             p_pass(0, k - 1)
             x_to_channels(k, 1)
             interleave_on_vector(k - 1)
-            if k >= 2:
-                scale_rows_on_gpsimd(k, 1)
+            if full:
+                scale_on_vector(k, (3,))
+                neg_column = factor_for_gpsimd(2)
             else:
-                scale_rows(k, 1)
+                scale_on_vector(k, (2, 3))
             if k + 2 < B:
                 mask_grad(k + 2, 0, (0,))
             else:
                 nc.vector.tensor_scalar(
                     out=mask[:], in0=adj_rows[:], scalar1=bias[:], scalar2=0.0, op0=ALU.add, op1=ALU.is_gt
                 )
+            if full:
+                scale_on_gpsimd(k, 2, neg_column)
             transpose_dz1(k, 0)
             p_pass(1, k - 1)
-            transpose_dz1(k, 1, WARM[1])
-            if k >= 2:
+            transpose_dz1(k, 1, WARM_STEP)
+            if full:
                 finish_dx(k - 2, 2)
                 finish_dx(k - 2, 3)
             quantize_grad(k + 1)
             if k + 2 < B:
                 mask_grad(k + 2, 0, (1,))
 
+
+        w_t = keep.tile([P, T, N], F32, name="w_t")
+        p_d = rows_f32("p_d", [P, T, N])
+        p_wd = keep.tile([P, T, N], F32, name="p_wd")
+        half_d2 = keep.tile([P, T], F32, name="half_d2")
         col_sums = keep.tile([P, T], F32, name="col_sums")
         row_sums = keep.tile([P, T], F32, name="row_sums")
         both_sums = keep.tile([P, T], F32, name="both_sums")
         shift = keep.tile([P, T], F32, name="shift")
-        p_d = work.tile([P, T, N], F32, name="p_d", tag="rows_f32", bufs=5)
-        p_wd = keep.tile([P, T, N], F32, name="p_wd")
-        unused = keep.tile([P, P], F32, name="unused")
-        pd_banks = {}
-
-        def scale_p(s):
-            nc.scalar.activation(out=p_d[:, s, :], in_=p_banks[s][:], func=ACT.Copy, scale=d_rows[:, s : s + 1])
-
-        def weigh_p(s):
-            nc.vector.scalar_tensor_tensor(
-                out=p_wd[:, s, :],
-                in0=p_banks[s][:],
-                scalar=d_rows[:, s : s + 1],
-                in1=w_t[:, s, :],
-                op0=ALU.mult,
-                op1=ALU.mult,
-                accum_out=col_sums[:, s : s + 1],
-            )
-
-        def sum_rows():
-            parts = bank("row_parts", [P, T, P])
-            for r in range(T):
-                for s in range(T):
-                    nc.tensor.matmul(
-                        out=parts[:, r, :],
-                        lhsT=p_wd[:, s, r * P : (r + 1) * P],
-                        rhs=ident[:],
-                        start=s == 0,
-                        stop=s == T - 1,
-                        is_transpose=True,
-                    )
-            return parts
-
-        def transpose_back(r):
-            pd_banks[r] = held_bank("pd_held", [P, T, P]) if r < P_IN_LOOP else bank("pd_acc", [P, T, P])
-            for s in range(T):
-                nc.tensor.transpose(pd_banks[r][:, s, :], p_d[:, s, r * P : (r + 1) * P], ident[:])
 
         quantize_dz1(last - 2)
-        copy_dz1_t(last - 1, 0)
-        copy_dz1_t(last - 1, 1)
+        copy_dz1_t(last - 1)
         first_product(last, 0)
         first_product(last, 1)
         mix_nodes(last - 2, 0)
@@ -491,30 +483,27 @@ def tile_brainfunctionalconnectivityfeatureextrac_pa_v_kernel(
         x_to_channels(last, 1)
         quantize_x_t(last - 1)
         nc.vector.scalar_tensor_tensor(
-            out=factor[:], in0=d_rows[:], scalar=-0.5, in1=d_rows[:], op0=ALU.mult, op1=ALU.mult
+            out=half_d2[:], in0=d_rows[:], scalar=-0.5, in1=d_rows[:], op0=ALU.mult, op1=ALU.mult
         )
         finish_dx(last - 2, 0)
         quantize_dz1_t(last - 1)
-        scale_rows(last, 0)
-        transpose_dz1(last, 0)
-        mix_nodes(last - 2, 2)
-        p_pass(0, last - 1)
-        finish_dx(last - 2, 1)
-        scale_rows(last, 1)
-        transpose_dz1(last, 1)
-        mix_nodes(last - 2, 3)
-        p_pass(1, last - 1)
-        copy_dz1_t(last, 0)
-        copy_dz1_t(last, 1)
+        for h in range(2):
+            scale_on_vector(last, (2 * h, 2 * h + 1))
+            transpose_dz1(last, h)
+            mix_nodes(last - 2, 2 + h)
+            p_pass(h, last - 1)
+            if h == 0:
+                finish_dx(last - 2, 1)
+        copy_dz1_t(last)
         interleave_on_scalar(last - 1, 0)
         interleave_on_scalar(last - 1, 1)
         interleave_on_vector(last - 1)
         finish_dx(last - 2, 2)
         quantize_x_t(last)
         finish_dx(last - 2, 3)
-        transpose_w(0)
-        transpose_w(1)
-        transpose_w(2)
+
+        for s in range(T - 1):
+            transpose_w(s)
         for b in range(EARLY_PASSES):
             p_pass(2, b)
         quantize_dz1_t(last)
@@ -526,7 +515,7 @@ def tile_brainfunctionalconnectivityfeatureextrac_pa_v_kernel(
             p_pass(2, b)
         mix_nodes(last - 1, 1)
         interleave_on_scalar(last, 0)
-        transpose_w(3)
+        transpose_w(T - 1)
         interleave_on_scalar(last, 1)
         weigh_p(0)
         weigh_p(1)
@@ -542,28 +531,24 @@ def tile_brainfunctionalconnectivityfeatureextrac_pa_v_kernel(
         finish_dx(last - 1, 2)
         quantize_dz1(last)
         mix_nodes(last, 0)
-        weigh_p(3)
-        for s in range(T):
-            scale_p(s)
-        row_parts = sum_rows()
-        for r in range(T):
-            nc.scalar.activation(
-                out=unused[:], in_=row_parts[:, r, :], func=ACT.Copy, accum_out=row_sums[:, r : r + 1]
-            )
         finish_dx(last - 1, 3)
         mix_nodes(last, 1)
-        transpose_back(0)
+        weigh_p(3)
+
+        for s in range(T):
+            scale_p(s)
+        row_parts = add_row_tiles()
         finish_dx(last, 0)
         mix_nodes(last, 2)
-        transpose_back(1)
         finish_dx(last, 1)
         mix_nodes(last, 3)
-        transpose_back(2)
-        transpose_back(3)
-        nc.vector.tensor_tensor(out=both_sums[:], in0=col_sums[:], in1=row_sums[:], op=ALU.add)
+        for r in range(T):
+            transpose_back(r)
+        nc.vector.tensor_reduce(out=row_sums[:], in_=row_parts[:], axis=mybir.AxisListType.X, op=ALU.add)
         finish_dx(last, 2)
-        nc.vector.tensor_tensor(out=shift[:], in0=both_sums[:], in1=factor[:], op=ALU.mult)
+        nc.vector.tensor_tensor(out=both_sums[:], in0=col_sums[:], in1=row_sums[:], op=ALU.add)
         finish_dx(last, 3)
+        nc.vector.tensor_tensor(out=shift[:], in0=both_sums[:], in1=half_d2[:], op=ALU.mult)
         for r in range(T):
             nc.vector.scalar_tensor_tensor(
                 out=p_wd[:, r, :],

@@ -28,8 +28,6 @@ STEADY_SHARE, EDGE_SHARE = 16, 64
 
 EARLY_PASSES = 4
 
-WARM_START, WARM_FILL, WARM_STEP = 5, 3, 1
-
 
 def tile_brainfunctionalconnectivityfeatureextrac_pa_v_kernel(
     tc, x, adj, adj_bias, cheb_w, brelu_bias, z, d, grad_out, out_0, out_1
@@ -80,16 +78,8 @@ def tile_brainfunctionalconnectivityfeatureextrac_pa_v_kernel(
 
         ident_bf = keep.tile([P, P], BF16, name="ident_bf")
         make_identity(nc, ident_bf[:])
-        zeros = keep.tile([P, N], BF16, name="zeros")
-        nc.gpsimd.memset(zeros[:], 0.0)
         ident = keep.tile([P, P], F32, name="ident")
         make_identity(nc, ident[:])
-
-        def keep_warm(acc, count):
-            for n in range(count):
-                nc.tensor.matmul(
-                    out=acc[:].rearrange("p s m -> p (s m)"), lhsT=ident_bf[:], rhs=zeros[:], start=True, stop=True
-                )
 
         g_half, z_half, x_rows, sorted_half = {}, {}, {}, {}
         g_grouped, zt_grouped, xt_grouped, a_grouped = {}, {}, {}, {}
@@ -132,10 +122,9 @@ def tile_brainfunctionalconnectivityfeatureextrac_pa_v_kernel(
                     op1=ALU.mult,
                 )
 
-        def sorted_to_grouped(key, grouped, h, warm=0):
+        def sorted_to_grouped(key, grouped, h):
             words = sorted_half[key][:].bitcast(F32)
             acc = ring_bank("sorted_t", [P, 4, P])
-            keep_warm(acc, warm)
             for t in range(2):
                 for u in range(2):
                     first = (2 * u + t) * P
@@ -145,10 +134,10 @@ def tile_brainfunctionalconnectivityfeatureextrac_pa_v_kernel(
                 in_=acc[:].rearrange("q (t u) p -> q t p u", u=2),
             )
 
-        def grad_to_features(b, h, warm=0):
+        def grad_to_features(b, h):
             if h == 0:
                 g_grouped[b] = grouped_tile("g_grouped")
-            sorted_to_grouped((b, h), g_grouped[b], h, warm)
+            sorted_to_grouped((b, h), g_grouped[b], h)
 
         def quantize_grad(b):
             g_mx[b] = mx_operand(work, "g", 2)
@@ -198,10 +187,9 @@ def tile_brainfunctionalconnectivityfeatureextrac_pa_v_kernel(
             words = grouped[:].bitcast(F32).rearrange("q (p h s) -> q h p s", h=2, s=4)
             nc.scalar.copy(out=words[:, h], in_=acc[:].rearrange("q s p -> q p s"))
 
-        def transpose_dz1(b, h, warm=0):
+        def transpose_dz1(b, h):
             words = dz1[b][:].bitcast(F32)
             z_banks[b, h] = ring_bank("dz1_t", [P, 4, P])
-            keep_warm(z_banks[b, h], warm)
             for s in range(4):
                 first = (4 * h + s) * P
                 nc.tensor.transpose(z_banks[b, h][:, s, :], words[:, first : first + P], ident[:])
@@ -336,8 +324,6 @@ def tile_brainfunctionalconnectivityfeatureextrac_pa_v_kernel(
         load_gz(2)
         load_x(1)
 
-        warm_bank = held_bank("warm", [P, 4, P])
-        keep_warm(warm_bank, WARM_START)
         w1_flat = w1_rows[:].rearrange("p r h -> p (r h)")
         w1_grouped = grouped_tile("a_grouped")
         for h in range(2):
@@ -347,10 +333,8 @@ def tile_brainfunctionalconnectivityfeatureextrac_pa_v_kernel(
             )
         for h in range(2):
             sorted_to_grouped(("w1", h), w1_grouped, h)
-        keep_warm(warm_bank, WARM_FILL)
         mask_grad(0, 0)
         grad_to_features(0, 0)
-        keep_warm(warm_bank, WARM_FILL)
         w1_mx = mx_operand(keep, "w1", 1)
         quantize(w1_mx, E4M3, w1_grouped)
         mask_grad(0, 1)
@@ -368,7 +352,6 @@ def tile_brainfunctionalconnectivityfeatureextrac_pa_v_kernel(
         first_product(0, 3)
         mask_grad(1, 1)
         grad_to_features(1, 1)
-        keep_warm(warm_bank, WARM_FILL)
         x_to_channels(0, 0)
         x_to_channels(0, 1)
         scale_on_vector(0, range(T))
@@ -423,7 +406,7 @@ def tile_brainfunctionalconnectivityfeatureextrac_pa_v_kernel(
             if full:
                 scale_on_gpsimd(k, 0, neg_column)
             interleave_on_scalar(k - 1, 0)
-            grad_to_features(k + 1, 1, WARM_STEP)
+            grad_to_features(k + 1, 1)
             interleave_on_scalar(k - 1, 1)
             x_to_channels(k, 0)
             if full:
@@ -453,7 +436,7 @@ def tile_brainfunctionalconnectivityfeatureextrac_pa_v_kernel(
                 scale_on_gpsimd(k, 2, neg_column)
             transpose_dz1(k, 0)
             p_pass(1, k - 1)
-            transpose_dz1(k, 1, WARM_STEP)
+            transpose_dz1(k, 1)
             if full:
                 finish_dx(k - 2, 2)
                 finish_dx(k - 2, 3)

from contextlib import ExitStack

import concourse.mybir as mybir
from concourse.masks import make_identity

B = 8
N = 512
P = 128
T = 4
HALF = 2 * N
RUN = 16

FLOPS = 3 * 2 * B * N * N * N
BYTES = B * N * N * (2 + 2 + 4 + 4) + N * N * (2 + 2 + 4) + N * 4 + 2

F32 = mybir.dt.float32
BF16 = mybir.dt.bfloat16
U32 = mybir.dt.uint32
U8 = mybir.dt.uint8
E4M3 = mybir.dt.float8_e4m3fn_x4
E5M2 = mybir.dt.float8_e5m2_x4
ALU = mybir.AluOpType
ACT = mybir.ActivationFunctionType

HELD_BANKS, U_BANKS, RING_BANKS = 2, 2, 4

STEADY_SHARE, EDGE_SHARE = 16, 64

EARLY_PASSES = 4


def tile_brainfunctionalconnectivityfeatureextrac_pa_v_kernel(
    tc, x, adj, adj_bias, cheb_w, brelu_bias, z, d, grad_out, out_0, out_1
):
    nc = tc.nc
    last = B - 1
    with ExitStack() as ctx:
        keep = ctx.enter_context(tc.tile_pool(name="keep", bufs=1))
        load = ctx.enter_context(tc.tile_pool(name="load", bufs=3))
        work = ctx.enter_context(tc.tile_pool(name="work", bufs=2))
        psum = ctx.enter_context(tc.psum_pool(name="psum", bufs=1))
        ctx.enter_context(tc.manual_schedule())

        def ring_bank(name, shape, dtype=F32):
            return psum.tile(shape, dtype, name=name, tag="ring", bufs=RING_BANKS)

        def held_bank(name, shape):
            return psum.tile(shape, F32, name=name, tag="held", bufs=HELD_BANKS)

        def rows_f32(name, shape):
            return work.tile(shape, F32, name=name, tag="rows_f32", bufs=5)

        def grouped_tile(tag):
            return work.tile([P, N * T], BF16, name=tag, tag=tag, bufs=2, align_bytes=64)

        def mx_operand(pool, tag, bufs):
            codes = pool.tile([P, N], U32, name=tag + "_codes", tag=tag + "_codes", bufs=bufs, align_bytes=64)
            scales = pool.tile([P, N], U8, name=tag + "_scales", tag=tag + "_scales", bufs=bufs, align_bytes=64)
            return codes, scales

        def quantize(operand, fmt, grouped):
            nc.vector.quantize_mx(out=operand[0][:].bitcast(fmt), scales=operand[1][:], in_=grouped[:])

        def mx_pass(acc, lhs, lhs_fmt, row_tile, rhs, rhs_fmt, start, stop):
            cols = slice(row_tile * P, (row_tile + 1) * P)
            nc.tensor.matmul_mx(
                out=acc[:],
                lhsT=lhs[0][:, cols].bitcast(lhs_fmt),
                lhsT_scale=lhs[1][:, cols],
                rhs=rhs[0][:].bitcast(rhs_fmt),
                rhs_scale=rhs[1][:],
                start=start,
                stop=stop,
            )

        def tile_cols(t):
            return slice(t * N, (t + 1) * N)

        ident_bf = keep.tile([P, P], BF16, name="ident_bf")
        make_identity(nc, ident_bf[:])
        ident = keep.tile([P, P], F32, name="ident")
        make_identity(nc, ident[:])

        g_half, z_half, x_rows, sorted_half = {}, {}, {}, {}
        g_grouped, zt_grouped, xt_grouped, a_grouped = {}, {}, {}, {}
        g_mx, zt_mx, xt_mx, a_mx = {}, {}, {}, {}
        dt1, dz1, z_banks, u_banks, p_banks, pd_banks = {}, {}, {}, {}, {}, {}


        def load_gz(b):
            for h in range(2):
                cols = slice(h * HALF, (h + 1) * HALF)
                g_half[b, h] = load.tile([P, HALF], BF16, name="g_half", tag="g_half", bufs=6)
                nc.sync.dma_start(out=g_half[b, h][:], in_=grad_out[b].rearrange("(p t) h -> p (t h)", t=T)[:, cols])
                z_half[b, h] = load.tile([P, HALF], F32, name="z_half", tag="z_half", bufs=6)
                nc.sync.dma_start(out=z_half[b, h][:], in_=z[b].rearrange("(p t) h -> p (t h)", t=T)[:, cols])

        def load_x(b):
            x_rows[b] = load.tile([P, N * T], BF16, name="x_rows", tag="x_rows", bufs=3)
            nc.sync.dma_start(out=x_rows[b][:], in_=x[b].rearrange("(p t) c -> p (t c)", t=T))


        def unsorted_view(ap):
            return ap.rearrange("p (a u r) -> p u a r", u=2, r=RUN)

        def sorted_view(ap):
            return ap.rearrange("p (u a r) -> p u a r", u=2, r=RUN)

        def new_sorted_half(key):
            sorted_half[key] = work.tile([P, HALF], BF16, name="sorted_half", tag="sorted_half", bufs=4)

        def mask_grad(b, h, parts=(0, 1)):
            for u in parts:
                if u == 0:
                    new_sorted_half((b, h))
                nc.vector.scalar_tensor_tensor(
                    out=sorted_view(sorted_half[b, h][:])[:, u],
                    in0=unsorted_view(z_half[b, h][:])[:, u],
                    scalar=0.0,
                    in1=unsorted_view(g_half[b, h][:])[:, u],
                    op0=ALU.is_gt,
                    op1=ALU.mult,
                )

        def sorted_to_grouped(key, grouped, h):
            words = sorted_half[key][:].bitcast(F32)
            acc = ring_bank("sorted_t", [P, 4, P])
            for t in range(2):
                for u in range(2):
                    first = (2 * u + t) * P
                    nc.tensor.transpose(acc[:, 2 * t + u, :], words[:, first : first + P], ident[:])
            nc.scalar.copy(
                out=grouped[:].bitcast(F32)[:, tile_cols(h)].rearrange("q (t p u) -> q t p u", t=2, u=2),
                in_=acc[:].rearrange("q (t u) p -> q t p u", u=2),
            )

        def grad_to_features(b, h):
            if h == 0:
                g_grouped[b] = grouped_tile("g_grouped")
            sorted_to_grouped((b, h), g_grouped[b], h)

        def quantize_grad(b):
            g_mx[b] = mx_operand(work, "g", 2)
            quantize(g_mx[b], E5M2, g_grouped[b])

        def quantize_first_grad(h):
            if h == 0:
                g_mx[0] = mx_operand(work, "g", 2)
            cols = slice(h * 2 * P, (h + 1) * 2 * P)
            nc.vector.quantize_mx(
                out=g_mx[0][0][:, cols].bitcast(E5M2),
                scales=g_mx[0][1][:, cols],
                in_=g_grouped[0][:, h * HALF : (h + 1) * HALF],
            )


        def first_product(b, t):
            if t == 0:
                dt1[b] = rows_f32("dt1", [P, T * N])
                dz1[b] = work.tile([P, T * N], BF16, name="dz1", tag="dz1", bufs=3)
            acc = ring_bank("dt1_acc", [P, N])
            mx_pass(acc, g_mx[b], E5M2, t, w1_mx, E4M3, True, True)
            nc.scalar.copy(out=dt1[b][:, tile_cols(t)], in_=acc[:])

        def scale_views(b, t):
            dst = dz1[b][:, tile_cols(t)].rearrange("p (u w e) -> p u w e", u=2, e=2)
            src = dt1[b][:, tile_cols(t)].rearrange("p (w u e) -> p u w e", u=2, e=2)
            return dst, src

        def scale_on_vector(b, tiles):
            for t in tiles:
                dst, src = scale_views(b, t)
                nc.vector.tensor_scalar(out=dst, in0=src, scalar1=neg_d[:, t : t + 1], scalar2=None, op0=ALU.mult)


        def factor_for_gpsimd(t):
            neg_column = work.tile([P, 1], F32, name="neg_column", tag="neg_column", bufs=2)
            nc.vector.tensor_scalar(out=neg_column[:], in0=d_by4[:, t : t + 1], scalar1=-1.0, scalar2=None, op0=ALU.mult)
            return neg_column

        def scale_on_gpsimd(b, t, neg_column):
            dst, src = scale_views(b, t)
            nc.gpsimd.tensor_scalar(out=dst, in0=src, scalar1=neg_column[:], scalar2=0.0, op0=ALU.mult, op1=ALU.add)


        def copy_nodes_in_order(grouped, h, acc):
            words = grouped[:].bitcast(F32).rearrange("q (p h s) -> q h p s", h=2, s=4)
            nc.scalar.copy(out=words[:, h], in_=acc[:].rearrange("q s p -> q p s"))

        def transpose_dz1(b, h):
            words = dz1[b][:].bitcast(F32)
            z_banks[b, h] = ring_bank("dz1_t", [P, 4, P])
            for s in range(4):
                first = (4 * h + s) * P
                nc.tensor.transpose(z_banks[b, h][:, s, :], words[:, first : first + P], ident[:])

        def copy_dz1_t(b):
            zt_grouped[b] = grouped_tile("zt_grouped")
            for h in range(2):
                copy_nodes_in_order(zt_grouped[b], h, z_banks[b, h])

        def quantize_dz1_t(b):
            zt_mx[b] = mx_operand(keep, "zt", B)
            quantize(zt_mx[b], E5M2, zt_grouped[b])

        def x_to_channels(b, h):
            words = x_rows[b][:].bitcast(F32)
            acc = ring_bank("x_t", [P, 4, P])
            for t in range(2):
                for u in range(2):
                    first = (2 * h + t) * 2 * P
                    nc.tensor.transpose(acc[:, 2 * t + u, :], words[:, first + u : first + 2 * P : 2], ident[:])
            if h == 0:
                xt_grouped[b] = grouped_tile("xt_grouped")
            copy_nodes_in_order(xt_grouped[b], h, acc)

        def quantize_x_t(b):
            xt_mx[b] = mx_operand(keep, "xt", B)
            quantize(xt_mx[b], E4M3, xt_grouped[b])

        def p_pass(s, b):
            if b == 0:
                p_banks[s] = held_bank("p_held", [P, N]) if s < HELD_BANKS else ring_bank("p_acc", [P, N])
            mx_pass(p_banks[s], xt_mx[b], E4M3, s, zt_mx[b], E5M2, b == 0, b == last)


        def vector_share(b):
            if b == last:
                return 0
            return EDGE_SHARE if b in (0, last - 1) else STEADY_SHARE

        def interleave_views(b, first, end):
            src = dz1[b][:].rearrange("p (t u w e) -> p u w t e", t=T, u=2, e=2)[:, :, first:end]
            dst = a_grouped[b][:].rearrange("p (w u e t) -> p u w t e", t=T, u=2, e=2)[:, :, first:end]
            return dst, src

        def interleave_on_scalar(b, h):
            if h == 0:
                a_grouped[b] = grouped_tile("a_grouped")
            cuts = (vector_share(b), (vector_share(b) + P) // 2, P)
            dst, src = interleave_views(b, cuts[h], cuts[h + 1])
            nc.scalar.copy(out=dst, in_=src)

        def interleave_on_vector(b):
            dst, src = interleave_views(b, 0, vector_share(b))
            nc.vector.tensor_copy(out=dst, in_=src)

        def quantize_dz1(b):
            a_mx[b] = mx_operand(work, "a", 2)
            quantize(a_mx[b], E5M2, a_grouped[b])

        def mix_nodes(b, t):
            u_banks[b, t] = psum.tile([P, N], F32, name="u_acc", tag="u", bufs=U_BANKS)
            mx_pass(u_banks[b, t], w_mx, E4M3, t, a_mx[b], E5M2, True, True)

        def finish_dx(b, t):
            nc.vector.scalar_tensor_tensor(
                out=dt1[b][:, tile_cols(t)],
                in0=u_banks[b, t][:],
                scalar=d_by4[:, t : t + 1],
                in1=dt1[b][:, tile_cols(t)],
                op0=ALU.mult,
                op1=ALU.add,
            )
            if t % 2 == 1 or b == last:
                cols = tile_cols(t) if b == last else slice((t - 1) * N, (t + 1) * N)
                nc.sync.dma_start(out=out_0[b].rearrange("(p t) c -> p (t c)", t=T)[:, cols], in_=dt1[b][:, cols])


        def transpose_w(s):
            acc = ring_bank("adj_t", [P, T, P], BF16)
            for r in range(T):
                nc.tensor.transpose(acc[:, r, :], adj_rows[:, r, s * P : (s + 1) * P], ident_bf[:])
            nc.scalar.activation(
                out=w_t[:, s, :], in_=acc[:].rearrange("p r m -> p (r m)"), func=ACT.Relu, bias=bias[:]
            )

        def weigh_p(s):
            nc.vector.scalar_tensor_tensor(
                out=p_wd[:, s, :],
                in0=p_banks[s][:],
                scalar=d_rows[:, s : s + 1],
                in1=w_t[:, s, :],
                op0=ALU.mult,
                op1=ALU.mult,
                accum_out=col_sums[:, s : s + 1],
            )

        def scale_p(s):
            nc.scalar.activation(out=p_d[:, s, :], in_=p_banks[s][:], func=ACT.Copy, scale=d_rows[:, s : s + 1])

        def add_row_tiles():
            parts = ring_bank("row_parts", [P, T, P])
            for r in range(T):
                for s in range(T):
                    nc.tensor.matmul(
                        out=parts[:, r, :],
                        lhsT=p_wd[:, s, r * P : (r + 1) * P],
                        rhs=ident[:],
                        start=s == 0,
                        stop=s == T - 1,
                        is_transpose=True,
                    )
            return parts

        def transpose_back(r):
            pd_banks[r] = held_bank("pd_held", [P, T, P]) if r < HELD_BANKS else ring_bank("pd_acc", [P, T, P])
            for s in range(T):
                nc.tensor.transpose(pd_banks[r][:, s, :], p_d[:, s, r * P : (r + 1) * P], ident[:])


        w1_rows = keep.tile([P, T, N], BF16, name="w1_rows")
        nc.sync.dma_start(out=w1_rows[:], in_=cheb_w.rearrange("(r p k) h -> k p r h", k=2, p=P)[1])
        load_gz(0)
        d_by4 = keep.tile([P, T], F32, name="d_by4")
        nc.sync.dma_start(out=d_by4[:], in_=d.rearrange("(p t) -> p t", t=T))
        load_gz(1)
        bias = keep.tile([P, 1], BF16, name="bias")
        with nc.allow_non_contiguous_dma(reason="one number for every partition"):
            nc.sync.dma_start(out=bias[:], in_=adj_bias.partition_broadcast(P))
        adj_by4 = keep.tile([P, T * N], BF16, name="adj_by4")
        nc.sync.dma_start(out=adj_by4[:], in_=adj.rearrange("(p t) j -> p (t j)", t=T))
        load_x(0)
        load_gz(2)
        load_x(1)

        w1_flat = w1_rows[:].rearrange("p r h -> p (r h)")
        w1_grouped = grouped_tile("a_grouped")
        for h in range(2):
            new_sorted_half(("w1", h))
            nc.vector.tensor_copy(
                out=sorted_view(sorted_half["w1", h][:]), in_=unsorted_view(w1_flat[:, h * HALF : (h + 1) * HALF])
            )
        for h in range(2):
            sorted_to_grouped(("w1", h), w1_grouped, h)
        mask_grad(0, 0)
        grad_to_features(0, 0)
        w1_mx = mx_operand(keep, "w1", 1)
        quantize(w1_mx, E4M3, w1_grouped)
        mask_grad(0, 1)
        grad_to_features(0, 1)
        neg_d = keep.tile([P, T], F32, name="neg_d")
        nc.vector.tensor_scalar(out=neg_d[:], in0=d_by4[:], scalar1=-1.0, scalar2=None, op0=ALU.mult)

        quantize_first_grad(0)
        first_product(0, 0)
        first_product(0, 1)
        mask_grad(1, 0)
        quantize_first_grad(1)
        grad_to_features(1, 0)
        first_product(0, 2)
        first_product(0, 3)
        mask_grad(1, 1)
        grad_to_features(1, 1)
        x_to_channels(0, 0)
        x_to_channels(0, 1)
        scale_on_vector(0, range(T))
        transpose_dz1(0, 0)
        transpose_dz1(0, 1)
        quantize_grad(1)
        w_grouped = grouped_tile("a_grouped")
        nc.vector.tensor_scalar(
            out=w_grouped[:].rearrange("p (s m t) -> p s m t", s=T, t=T),
            in0=adj_by4[:].rearrange("p (t m s) -> p s m t", s=T, t=T),
            scalar1=bias[:],
            scalar2=0.0,
            op0=ALU.add,
            op1=ALU.max,
        )
        mask_grad(2, 0)
        load_gz(3)

        w_mx = mx_operand(keep, "w", 1)
        adj_rows = keep.tile([P, T, N], BF16, name="adj_rows")
        d_rows = keep.tile([P, T], F32, name="d_rows")
        mask = keep.tile([P, T, N], BF16, name="mask")


        for k in range(1, last):
            full = k >= 2
            load_x(k + 1)
            if k + 3 < B:
                load_gz(k + 3)
            if k == 1:
                nc.sync.dma_start(out=adj_rows[:], in_=adj.rearrange("(r p) j -> p r j", p=P))
            if k == 2:
                with nc.allow_non_contiguous_dma(reason="one factor for each row"):
                    nc.sync.dma_start(out=d_rows[:], in_=d.rearrange("(r p) -> p r", p=P))
            if full:
                quantize_dz1(k - 2)
            copy_dz1_t(k - 1)
            first_product(k, 0)
            first_product(k, 1)
            if full:
                mix_nodes(k - 2, 0)
            grad_to_features(k + 1, 0)
            first_product(k, 2)
            if full:
                mix_nodes(k - 2, 1)
            first_product(k, 3)
            quantize_x_t(k - 1)
            mask_grad(k + 1, 1)
            if full:
                neg_column = factor_for_gpsimd(0)
            quantize_dz1_t(k - 1)
            if full:
                scale_on_gpsimd(k, 0, neg_column)
            interleave_on_scalar(k - 1, 0)
            grad_to_features(k + 1, 1)
            interleave_on_scalar(k - 1, 1)
            x_to_channels(k, 0)
            if full:
                finish_dx(k - 2, 0)
                finish_dx(k - 2, 1)
                mix_nodes(k - 2, 2)
                mix_nodes(k - 2, 3)
                scale_on_vector(k, (1,))
            else:
                quantize(w_mx, E4M3, w_grouped)
                scale_on_vector(k, (0, 1))
            p_pass(0, k - 1)
            x_to_channels(k, 1)
            interleave_on_vector(k - 1)
            if full:
                scale_on_vector(k, (3,))
                neg_column = factor_for_gpsimd(2)
            else:
                scale_on_vector(k, (2, 3))
            if k + 2 < B:
                mask_grad(k + 2, 0, (0,))
            else:
                nc.vector.tensor_scalar(
                    out=mask[:], in0=adj_rows[:], scalar1=bias[:], scalar2=0.0, op0=ALU.add, op1=ALU.is_gt
                )
            if full:
                scale_on_gpsimd(k, 2, neg_column)
            transpose_dz1(k, 0)
            p_pass(1, k - 1)
            transpose_dz1(k, 1)
            if full:
                finish_dx(k - 2, 2)
                finish_dx(k - 2, 3)
            quantize_grad(k + 1)
            if k + 2 < B:
                mask_grad(k + 2, 0, (1,))


        w_t = keep.tile([P, T, N], F32, name="w_t")
        p_d = rows_f32("p_d", [P, T, N])
        p_wd = keep.tile([P, T, N], F32, name="p_wd")
        half_d2 = keep.tile([P, T], F32, name="half_d2")
        col_sums = keep.tile([P, T], F32, name="col_sums")
        row_sums = keep.tile([P, T], F32, name="row_sums")
        both_sums = keep.tile([P, T], F32, name="both_sums")
        shift = keep.tile([P, T], F32, name="shift")

        quantize_dz1(last - 2)
        copy_dz1_t(last - 1)
        first_product(last, 0)
        first_product(last, 1)
        mix_nodes(last - 2, 0)
        first_product(last, 2)
        mix_nodes(last - 2, 1)
        first_product(last, 3)
        x_to_channels(last, 0)
        x_to_channels(last, 1)
        quantize_x_t(last - 1)
        nc.vector.scalar_tensor_tensor(
            out=half_d2[:], in0=d_rows[:], scalar=-0.5, in1=d_rows[:], op0=ALU.mult, op1=ALU.mult
        )
        finish_dx(last - 2, 0)
        quantize_dz1_t(last - 1)
        for h in range(2):
            scale_on_vector(last, (2 * h, 2 * h + 1))
            transpose_dz1(last, h)
            mix_nodes(last - 2, 2 + h)
            p_pass(h, last - 1)
            if h == 0:
                finish_dx(last - 2, 1)
        copy_dz1_t(last)
        interleave_on_scalar(last - 1, 0)
        interleave_on_scalar(last - 1, 1)
        interleave_on_vector(last - 1)
        finish_dx(last - 2, 2)
        quantize_x_t(last)
        finish_dx(last - 2, 3)

        for s in range(T - 1):
            transpose_w(s)
        for b in range(EARLY_PASSES):
            p_pass(2, b)
        quantize_dz1_t(last)
        p_pass(0, last)
        p_pass(1, last)
        quantize_dz1(last - 1)
        mix_nodes(last - 1, 0)
        for b in range(EARLY_PASSES, B):
            p_pass(2, b)
        mix_nodes(last - 1, 1)
        interleave_on_scalar(last, 0)
        transpose_w(T - 1)
        interleave_on_scalar(last, 1)
        weigh_p(0)
        weigh_p(1)
        finish_dx(last - 1, 0)
        for b in range(EARLY_PASSES):
            p_pass(3, b)
        mix_nodes(last - 1, 2)
        weigh_p(2)
        finish_dx(last - 1, 1)
        for b in range(EARLY_PASSES, B):
            p_pass(3, b)
        mix_nodes(last - 1, 3)
        finish_dx(last - 1, 2)
        quantize_dz1(last)
        mix_nodes(last, 0)
        finish_dx(last - 1, 3)
        mix_nodes(last, 1)
        weigh_p(3)

        for s in range(T):
            scale_p(s)
        row_parts = add_row_tiles()
        finish_dx(last, 0)
        mix_nodes(last, 2)
        finish_dx(last, 1)
        mix_nodes(last, 3)
        for r in range(T):
            transpose_back(r)
        nc.vector.tensor_reduce(out=row_sums[:], in_=row_parts[:], axis=mybir.AxisListType.X, op=ALU.add)
        finish_dx(last, 2)
        nc.vector.tensor_tensor(out=both_sums[:], in0=col_sums[:], in1=row_sums[:], op=ALU.add)
        finish_dx(last, 3)
        nc.vector.tensor_tensor(out=shift[:], in0=both_sums[:], in1=half_d2[:], op=ALU.mult)
        for r in range(T):
            nc.vector.scalar_tensor_tensor(
                out=p_wd[:, r, :],
                in0=pd_banks[r][:].rearrange("p s m -> p (s m)"),
                scalar=shift[:, r : r + 1],
                in1=mask[:, r, :],
                op0=ALU.add,
                op1=ALU.mult,
            )
            nc.sync.dma_start(out=out_1[r * P : (r + 1) * P, :], in_=p_wd[:, r, :])
